import numpy as np
import ml_dtypes


def mxq(x, axis, fmt="e4m3"):
    dtype, down = {"e4m3": (ml_dtypes.float8_e4m3fn, 7), "e5m2": (ml_dtypes.float8_e5m2, 14)}[fmt]
    v = np.moveaxis(np.asarray(x, np.float32).astype(ml_dtypes.bfloat16).astype(np.float64), axis, -1)
    blocks = v.reshape(v.shape[:-1] + (-1, 32))
    amax = np.abs(blocks).max(-1, keepdims=True)
    byte = np.maximum(np.where(amax > 0, np.frexp(amax)[1] - 1 + 127, 0) - down, 1)
    scale = np.exp2(byte - 127.0)
    codes = (blocks / scale).astype(np.float32).astype(dtype).astype(np.float64)
    return np.moveaxis((codes * scale).reshape(v.shape), -1, axis)


WIDE = False


def mx_kscale(k):
    if not WIDE:
        return np.ones(k)
    levels = np.array([10, -10, 5, -5, 0])
    a = np.random.permutation(np.resize(levels, k // 512 * 4)).reshape(k // 512, 4)
    idx = np.arange(k)
    return np.exp2(a[idx // 512, idx % 128 // 32])


BF16 = ml_dtypes.bfloat16


def bf(x):
    return np.asarray(x, np.float32).astype(BF16)


def f64(x):
    return np.asarray(x).astype(np.float64)


B, S, H, HO, E = 4, 128, 1024, 1024, 8


def kahan_sum_last(x):
    s = np.zeros_like(x[..., 0])
    c = np.zeros_like(s)
    for i in range(x.shape[-1]):
        y = x[..., i] - c
        t = s + y
        c = (t - s) - y
        s = t
    return s


def setup_inputs():
    s = mx_kscale(H)
    return {"hidden_states": bf(np.random.standard_normal((B, S, H)) * s),
            "op_logits": bf(np.random.standard_normal((B, S, E)) * 1.3),
            "We": bf(np.random.standard_normal((E, H, HO)) / np.sqrt(H) / s[None, :, None]),
            "be": bf(np.random.standard_normal((E, HO)) * 0.3)}


def reference(hidden_states, op_logits, We, be):
    l = f64(op_logits)
    ex = np.exp(l - l.max(-1, keepdims=True))
    op_w = ex / ex.sum(-1, keepdims=True)
    prod = mxq(f64(hidden_states), 2, "e4m3")[:, None] @ mxq(f64(We), 1, "e4m3")[None]
    expert_out = prod.transpose(0, 2, 1, 3) + f64(be)
    weighted = expert_out * op_w[:, :, :, None]
    return kahan_sum_last(np.moveaxis(weighted, 2, -1))

@@ -1,0 +1,205 @@
+import concourse.mybir as mybir
+from concourse.masks import make_identity
+
+F32 = mybir.dt.float32
+BF16 = mybir.dt.bfloat16
+U32 = mybir.dt.uint32
+U8 = mybir.dt.uint8
+FP8X4 = mybir.dt.float8_e4m3fn_x4
+ALU = mybir.AluOpType
+ACT = mybir.ActivationFunctionType
+AXIS = mybir.AxisListType
+
+P = 128
+PACK = 4
+K_PASS = P * PACK
+TOKENS = 512
+H = 1024
+HO = 1024
+E = 8
+PASSES = H // K_PASS
+TOKEN_TILES = TOKENS // P
+N_BLOCK = 512
+N_BLOCKS = HO // N_BLOCK
+UNITS = E * N_BLOCKS
+RUN = 4
+HELPER_COLS = 160
+GATE_PARTS = 3
+
+FLOPS = 2 * TOKENS * H * HO * E
+
+
+def tile_enhancedmathematicalreasoning_pa_kernel(tc, hidden_states, op_logits, We, be, out):
+    nc = tc.nc
+    x_rows = hidden_states.flatten_outer_dims().rearrange("(p i) k -> p i k", i=TOKEN_TILES)
+    logit_rows = op_logits.flatten_outer_dims().rearrange("(p i) e -> p i e", i=TOKEN_TILES)
+    out_rows = out.flatten_outer_dims().rearrange("(p i) n -> p i n", i=TOKEN_TILES)
+
+    with tc.tile_pool(name="keep", bufs=1) as keep, tc.tile_pool(name="w_in", bufs=6) as w_in, tc.tile_pool(
+        name="w_mx", bufs=3
+    ) as w_mx, tc.psum_pool(name="psum", bufs=8) as psum, tc.manual_schedule():
+        logits = keep.tile([P, TOKEN_TILES, E], BF16)
+        nc.sync.dma_start(out=logits[:], in_=logit_rows)
+        be_rows = keep.tile([P, HO], BF16)
+        nc.vector.memset(be_rows[:], 0.0)
+        for part in range(GATE_PARTS):
+            nc.sync.dma_start(out=be_rows[E * part : E * (part + 1), :], in_=be)
+        x_raw = keep.tile([P, TOKEN_TILES, H], BF16)
+        for half in range(2):
+            tiles = slice(2 * half, 2 * half + 2)
+            nc.sync.dma_start(out=x_raw[:, tiles, :], in_=x_rows[:, tiles, :])
+        identity_f32 = keep.tile([P, P], F32)
+        make_identity(nc, identity_f32[:])
+        identity_bf16 = keep.tile([P, P], BF16)
+        make_identity(nc, identity_bf16[:])
+
+        gate_parts = keep.tile([P, TOKEN_TILES, P], BF16)
+        nc.vector.memset(gate_parts[:], 0.0)
+        row_max = keep.tile([P, TOKEN_TILES], F32)
+        nc.vector.tensor_reduce(out=row_max[:], in_=logits[:], axis=AXIS.X, op=ALU.max)
+        shifted = keep.tile([P, TOKEN_TILES, E], F32)
+        nc.vector.tensor_tensor(
+            out=shifted[:],
+            in0=logits[:],
+            in1=row_max[:].unsqueeze(2).to_broadcast([P, TOKEN_TILES, E]),
+            op=ALU.subtract,
+        )
+        exps = keep.tile([P, TOKEN_TILES, E], F32)
+        nc.scalar.activation(out=exps[:], in_=shifted[:], func=ACT.Exp)
+        row_sum = keep.tile([P, TOKEN_TILES], F32)
+        nc.vector.tensor_reduce(out=row_sum[:], in_=exps[:], axis=AXIS.X, op=ALU.add)
+        inv_sum = keep.tile([P, TOKEN_TILES], F32)
+        nc.vector.reciprocal(out=inv_sum[:], in_=row_sum[:])
+        gate = keep.tile([P, TOKEN_TILES, E], F32)
+        nc.vector.tensor_tensor(
+            out=gate[:],
+            in0=exps[:],
+            in1=inv_sum[:].unsqueeze(2).to_broadcast([P, TOKEN_TILES, E]),
+            op=ALU.mult,
+        )
+        rest = gate
+        for part in range(GATE_PARTS):
+            kept = gate_parts[:, :, E * part : E * (part + 1)]
+            nc.vector.tensor_copy(out=kept, in_=rest[:])
+            if part < GATE_PARTS - 1:
+                smaller = keep.tile([P, TOKEN_TILES, E], F32, name="rest%d" % part)
+                nc.vector.tensor_tensor(out=smaller[:], in0=rest[:], in1=kept, op=ALU.subtract)
+                rest = smaller
+
+        x_words = x_raw[:].bitcast(F32).rearrange("p i (g q u) -> p i g u q", g=PASSES, u=2)
+        x_grouped = keep.tile([P, PASSES, TOKENS, PACK], BF16, align_bytes=64)
+        x_grouped_words = x_grouped[:].bitcast(F32)
+        for half in range(2):
+            for g in range(PASSES):
+                planes = psum.tile([P, 2, 2 * P], F32, tag="bank")
+                for u in range(2):
+                    for i in range(2):
+                        nc.tensor.transpose(
+                            planes[:, u, P * i : P * (i + 1)], x_words[:, 2 * half + i, g, u, :], identity_f32[:]
+                        )
+                copy = nc.vector.tensor_copy if g == 0 else nc.scalar.copy
+                copy(
+                    out=x_grouped_words[:, g, 2 * P * half : 2 * P * (half + 1), :],
+                    in_=planes[:].rearrange("p u r -> p r u"),
+                )
+        x_codes = keep.tile([P, PASSES, TOKENS], U32, align_bytes=64)
+        x_scales = keep.tile([P, PASSES, TOKENS], U8, align_bytes=64)
+        nc.vector.quantize_mx(
+            out=x_codes[:].rearrange("p g r -> p (g r)").bitcast(FP8X4),
+            scales=x_scales[:].rearrange("p g r -> p (g r)"),
+            in_=x_grouped[:].rearrange("p g r t -> p (g r t)"),
+        )
+
+        total = keep.tile([P, TOKEN_TILES, HO], F32)
+        grouped_of = {}
+        banks_of = {}
+
+        def regroup(unit):
+            e, j = divmod(unit, N_BLOCKS)
+            w_raw = w_in.tile([P, PASSES, PACK, N_BLOCK], BF16)
+            for g in range(PASSES):
+                nc.sync.dma_start(
+                    out=w_raw[:, g],
+                    in_=We[e, K_PASS * g : K_PASS * (g + 1), N_BLOCK * j : N_BLOCK * (j + 1)].rearrange(
+                        "(p t) n -> p t n", t=PACK
+                    ),
+                )
+            w_grouped = w_mx.tile([P, PASSES, N_BLOCK, PACK], BF16, align_bytes=64)
+            scalar_cols = slice(0, N_BLOCK - HELPER_COLS)
+            helper_cols = slice(N_BLOCK - HELPER_COLS, N_BLOCK)
+            for g in range(PASSES):
+                nc.scalar.copy(
+                    out=w_grouped[:, g, scalar_cols, :].rearrange("p (c i) t -> p c t i", i=RUN),
+                    in_=w_raw[:, g, :, scalar_cols].rearrange("p t (c i) -> p c t i", i=RUN),
+                )
+            nc.gpsimd.tensor_scalar(
+                out=w_grouped[:, :, helper_cols, :],
+                in0=w_raw[:, :, :, helper_cols].rearrange("p g t n -> p g n t"),
+                scalar1=1.0,
+                scalar2=0.0,
+                op0=ALU.mult,
+                op1=ALU.add,
+            )
+            grouped_of[unit] = w_grouped
+
+        def multiply(unit):
+            w_codes = w_mx.tile([P, PASSES, N_BLOCK], U32, align_bytes=64)
+            w_scales = w_mx.tile([P, PASSES, N_BLOCK], U8, align_bytes=64)
+            nc.vector.quantize_mx(
+                out=w_codes[:].rearrange("p g n -> p (g n)").bitcast(FP8X4),
+                scales=w_scales[:].rearrange("p g n -> p (g n)"),
+                in_=grouped_of[unit][:].rearrange("p g n t -> p (g n t)"),
+            )
+            banks_of[unit] = []
+            for i in range(TOKEN_TILES):
+                t_cols = slice(P * i, P * (i + 1))
+                product = psum.tile([P, N_BLOCK], F32, tag="bank")
+                for g in range(PASSES):
+                    nc.tensor.matmul_mx(
+                        out=product[:],
+                        lhsT=x_codes[:, g, t_cols].bitcast(FP8X4),
+                        lhsT_scale=x_scales[:, g, t_cols],
+                        rhs=w_codes[:, g, :].bitcast(FP8X4),
+                        rhs_scale=w_scales[:, g, :],
+                        start=(g == 0),
+                        stop=(g == PASSES - 1),
+                    )
+                banks_of[unit].append(product)
+
+        def add_up(unit):
+            e, j = divmod(unit, N_BLOCKS)
+            n_cols = slice(N_BLOCK * j, N_BLOCK * (j + 1))
+            for i in range(TOKEN_TILES):
+                nc.vector.scalar_tensor_tensor(
+                    out=total[:, i, n_cols],
+                    in0=banks_of[unit][i][:],
+                    scalar=gate[:, i, e : e + 1],
+                    in1=total[:, i, n_cols],
+                    op0=ALU.mult,
+                    op1=ALU.add,
+                )
+                if e == E - 1:
+                    nc.sync.dma_start(out=out_rows[:, i, n_cols], in_=total[:, i, n_cols])
+
+        regroup(0)
+
+        gate_t_bank = psum.tile([P, TOKEN_TILES, P], BF16, tag="bank")
+        for i in range(TOKEN_TILES):
+            nc.tensor.transpose(gate_t_bank[:, i, :], gate_parts[:, i, :], identity_bf16[:])
+        gate_t = keep.tile([P, TOKEN_TILES, P], BF16)
+        nc.vector.tensor_copy(out=gate_t[:], in_=gate_t_bank[:])
+        for j in range(N_BLOCKS):
+            n_cols = slice(N_BLOCK * j, N_BLOCK * (j + 1))
+            for i in range(TOKEN_TILES):
+                bias_bank = psum.tile([P, N_BLOCK], F32, tag="bank")
+                nc.tensor.matmul(bias_bank[:], lhsT=gate_t[:, i, :], rhs=be_rows[:, n_cols], start=True, stop=True)
+                copy = nc.vector.tensor_copy if i % 2 == 0 else nc.scalar.copy
+                copy(out=total[:, i, n_cols], in_=bias_bank[:])
+
+        for unit in range(UNITS):
+            if unit + 1 < UNITS:
+                regroup(unit + 1)
+            multiply(unit)
+            if unit >= 1:
+                add_up(unit - 1)
+        add_up(UNITS - 1)

@@ -23,7 +23,13 @@ N_BLOCK = 512
 N_BLOCKS = HO // N_BLOCK
 UNITS = E * N_BLOCKS
 RUN = 4
-HELPER_COLS = 160
+HELPER_COLS = 128
+TENSOR_COLS = 128
+HEAD_UNITS = 4
+HEAD_VECTOR_COLS = 288
+HEAD_HELPER_COLS = 96
+FIRST_VECTOR_COLS = 320
+BIAS_UNIT = 4
 GATE_PARTS = 3
 
 FLOPS = 2 * TOKENS * H * HO * E
@@ -36,25 +42,47 @@ def tile_enhancedmathematicalreasoning_pa_kernel(tc, hidden_states, op_logits, W
     out_rows = out.flatten_outer_dims().rearrange("(p i) n -> p i n", i=TOKEN_TILES)
 
     with tc.tile_pool(name="keep", bufs=1) as keep, tc.tile_pool(name="w_in", bufs=6) as w_in, tc.tile_pool(
-        name="w_mx", bufs=3
+        name="w_mx", bufs=4
     ) as w_mx, tc.psum_pool(name="psum", bufs=8) as psum, tc.manual_schedule():
-        logits = keep.tile([P, TOKEN_TILES, E], BF16)
-        nc.sync.dma_start(out=logits[:], in_=logit_rows)
-        be_rows = keep.tile([P, HO], BF16)
-        nc.vector.memset(be_rows[:], 0.0)
-        for part in range(GATE_PARTS):
-            nc.sync.dma_start(out=be_rows[E * part : E * (part + 1), :], in_=be)
         x_raw = keep.tile([P, TOKEN_TILES, H], BF16)
-        for half in range(2):
+        raw_of = {}
+        grouped_of = {}
+        banks_of = {}
+
+        def load_x(half):
             tiles = slice(2 * half, 2 * half + 2)
             nc.sync.dma_start(out=x_raw[:, tiles, :], in_=x_rows[:, tiles, :])
+
+        def load(unit):
+            e, j = divmod(unit, N_BLOCKS)
+            w_raw = w_in.tile([P, PASSES, PACK, N_BLOCK], BF16)
+            for g in range(PASSES):
+                nc.sync.dma_start(
+                    out=w_raw[:, g],
+                    in_=We[e, K_PASS * g : K_PASS * (g + 1), N_BLOCK * j : N_BLOCK * (j + 1)].rearrange(
+                        "(p t) n -> p t n", t=PACK
+                    ),
+                )
+            raw_of[unit] = w_raw
+
+        logits = keep.tile([P, TOKEN_TILES, E], BF16)
+        nc.sync.dma_start(out=logits[:], in_=logit_rows)
+        load_x(0)
+        load(0)
+        load_x(1)
+        load(1)
+        load(2)
         identity_f32 = keep.tile([P, P], F32)
         make_identity(nc, identity_f32[:])
         identity_bf16 = keep.tile([P, P], BF16)
         make_identity(nc, identity_bf16[:])
-
+        be_rows = keep.tile([P, HO], BF16)
+        nc.gpsimd.memset(be_rows[:], 0.0)
         gate_parts = keep.tile([P, TOKEN_TILES, P], BF16)
-        nc.vector.memset(gate_parts[:], 0.0)
+        nc.gpsimd.memset(gate_parts[:], 0.0)
+        for part in range(GATE_PARTS):
+            nc.sync.dma_start(out=be_rows[E * part : E * (part + 1), :], in_=be)
+
         row_max = keep.tile([P, TOKEN_TILES], F32)
         nc.vector.tensor_reduce(out=row_max[:], in_=logits[:], axis=AXIS.X, op=ALU.max)
         shifted = keep.tile([P, TOKEN_TILES, E], F32)
@@ -77,19 +105,15 @@ def tile_enhancedmathematicalreasoning_pa_kernel(tc, hidden_states, op_logits, W
             in1=inv_sum[:].unsqueeze(2).to_broadcast([P, TOKEN_TILES, E]),
             op=ALU.mult,
         )
-        rest = gate
-        for part in range(GATE_PARTS):
-            kept = gate_parts[:, :, E * part : E * (part + 1)]
-            nc.vector.tensor_copy(out=kept, in_=rest[:])
-            if part < GATE_PARTS - 1:
-                smaller = keep.tile([P, TOKEN_TILES, E], F32, name="rest%d" % part)
-                nc.vector.tensor_tensor(out=smaller[:], in0=rest[:], in1=kept, op=ALU.subtract)
-                rest = smaller
 
         x_words = x_raw[:].bitcast(F32).rearrange("p i (g q u) -> p i g u q", g=PASSES, u=2)
-        x_grouped = keep.tile([P, PASSES, TOKENS, PACK], BF16, align_bytes=64)
+        x_grouped = keep.tile([P, 2, PASSES, 2 * P, PACK], BF16, align_bytes=64)
         x_grouped_words = x_grouped[:].bitcast(F32)
-        for half in range(2):
+        x_codes = keep.tile([P, 2, PASSES, 2 * P], U32, align_bytes=64)
+        x_scales = keep.tile([P, 2, PASSES, 2 * P], U8, align_bytes=64)
+
+        def turn_x(half):
+            banks = []
             for g in range(PASSES):
                 planes = psum.tile([P, 2, 2 * P], F32, tag="bank")
                 for u in range(2):
@@ -97,52 +121,74 @@ def tile_enhancedmathematicalreasoning_pa_kernel(tc, hidden_states, op_logits, W
                         nc.tensor.transpose(
                             planes[:, u, P * i : P * (i + 1)], x_words[:, 2 * half + i, g, u, :], identity_f32[:]
                         )
-                copy = nc.vector.tensor_copy if g == 0 else nc.scalar.copy
-                copy(
-                    out=x_grouped_words[:, g, 2 * P * half : 2 * P * (half + 1), :],
-                    in_=planes[:].rearrange("p u r -> p r u"),
-                )
-        x_codes = keep.tile([P, PASSES, TOKENS], U32, align_bytes=64)
-        x_scales = keep.tile([P, PASSES, TOKENS], U8, align_bytes=64)
-        nc.vector.quantize_mx(
-            out=x_codes[:].rearrange("p g r -> p (g r)").bitcast(FP8X4),
-            scales=x_scales[:].rearrange("p g r -> p (g r)"),
-            in_=x_grouped[:].rearrange("p g r t -> p (g r t)"),
-        )
+                banks.append(planes)
+            return banks
+
+        def group_x(half, banks):
+            for g, copy in enumerate((nc.vector.tensor_copy, nc.scalar.copy)):
+                copy(out=x_grouped_words[:, half, g], in_=banks[g][:].rearrange("p u r -> p r u"))
+
+        def quantize_x(half):
+            nc.vector.quantize_mx(
+                out=x_codes[:, half].rearrange("p g r -> p (g r)").bitcast(FP8X4),
+                scales=x_scales[:, half].rearrange("p g r -> p (g r)"),
+                in_=x_grouped[:, half].rearrange("p g r t -> p (g r t)"),
+            )
 
         total = keep.tile([P, TOKEN_TILES, HO], F32)
-        grouped_of = {}
-        banks_of = {}
+
+        def tensor_cols(unit):
+            return TENSOR_COLS if unit > 0 else 0
+
+        def vector_cols(unit):
+            if unit == 0:
+                return FIRST_VECTOR_COLS
+            return HEAD_VECTOR_COLS if unit < HEAD_UNITS else 0
+
+        def helper_cols(unit):
+            return HEAD_HELPER_COLS if unit < HEAD_UNITS else HELPER_COLS
+
+        def copy_cols(copy, unit, cols):
+            for g in range(PASSES) if cols.stop > cols.start else ():
+                copy(
+                    out=grouped_of[unit][:, g, cols, :].rearrange("p (c i) t -> p c t i", i=RUN),
+                    in_=raw_of[unit][:, g, :, cols].rearrange("p t (c i) -> p c t i", i=RUN),
+                )
 
         def regroup(unit):
-            e, j = divmod(unit, N_BLOCKS)
-            w_raw = w_in.tile([P, PASSES, PACK, N_BLOCK], BF16)
-            for g in range(PASSES):
-                nc.sync.dma_start(
-                    out=w_raw[:, g],
-                    in_=We[e, K_PASS * g : K_PASS * (g + 1), N_BLOCK * j : N_BLOCK * (j + 1)].rearrange(
-                        "(p t) n -> p t n", t=PACK
-                    ),
+            grouped_of[unit] = w_mx.tile([P, PASSES, N_BLOCK, PACK], BF16, align_bytes=64, name="w_grouped")
+            helper_start = N_BLOCK - helper_cols(unit)
+            copy_cols(nc.scalar.copy, unit, slice(tensor_cols(unit) + vector_cols(unit), helper_start))
+            for passes in (slice(0, 1), slice(1, 2)) if unit < HEAD_UNITS else (slice(0, 2),):
+                nc.gpsimd.tensor_scalar(
+                    out=grouped_of[unit][:, passes, helper_start:, :],
+                    in0=raw_of[unit][:, passes, :, helper_start:].rearrange("p g t n -> p g n t"),
+                    scalar1=1.0,
+                    scalar2=0.0,
+                    op0=ALU.mult,
+                    op1=ALU.add,
                 )
-            w_grouped = w_mx.tile([P, PASSES, N_BLOCK, PACK], BF16, align_bytes=64)
-            scalar_cols = slice(0, N_BLOCK - HELPER_COLS)
-            helper_cols = slice(N_BLOCK - HELPER_COLS, N_BLOCK)
+
+        def regroup_on_tensor(unit):
+            bank = psum.tile([P, PASSES, TENSOR_COLS * PACK], BF16, tag="bank")
+            for g in range(PASSES):
+                nc.tensor.matmul(
+                    bank[:, g, :],
+                    lhsT=identity_bf16[:],
+                    rhs=raw_of[unit][:, g, :, :TENSOR_COLS].rearrange("p t n -> p n t"),
+                    start=True,
+                    stop=True,
+                )
             for g in range(PASSES):
                 nc.scalar.copy(
-                    out=w_grouped[:, g, scalar_cols, :].rearrange("p (c i) t -> p c t i", i=RUN),
-                    in_=w_raw[:, g, :, scalar_cols].rearrange("p t (c i) -> p c t i", i=RUN),
+                    out=grouped_of[unit][:, g, :TENSOR_COLS, :].rearrange("p n t -> p (n t)"), in_=bank[:, g, :]
                 )
-            nc.gpsimd.tensor_scalar(
-                out=w_grouped[:, :, helper_cols, :],
-                in0=w_raw[:, :, :, helper_cols].rearrange("p g t n -> p g n t"),
-                scalar1=1.0,
-                scalar2=0.0,
-                op0=ALU.mult,
-                op1=ALU.add,
-            )
-            grouped_of[unit] = w_grouped
 
-        def multiply(unit):
+        def regroup_on_vector(unit):
+            start = tensor_cols(unit)
+            copy_cols(nc.vector.tensor_copy, unit, slice(start, start + vector_cols(unit)))
+
+        def quantize(unit):
             w_codes = w_mx.tile([P, PASSES, N_BLOCK], U32, align_bytes=64)
             w_scales = w_mx.tile([P, PASSES, N_BLOCK], U8, align_bytes=64)
             nc.vector.quantize_mx(
@@ -150,56 +196,109 @@ def tile_enhancedmathematicalreasoning_pa_kernel(tc, hidden_states, op_logits, W
                 scales=w_scales[:].rearrange("p g n -> p (g n)"),
                 in_=grouped_of[unit][:].rearrange("p g n t -> p (g n t)"),
             )
-            banks_of[unit] = []
-            for i in range(TOKEN_TILES):
-                t_cols = slice(P * i, P * (i + 1))
+            return w_codes, w_scales
+
+        def multiply(unit, w_codes, w_scales, tiles=range(TOKEN_TILES)):
+            for i in tiles:
+                half, t_cols = i // 2, slice(P * (i % 2), P * (i % 2 + 1))
                 product = psum.tile([P, N_BLOCK], F32, tag="bank")
                 for g in range(PASSES):
                     nc.tensor.matmul_mx(
                         out=product[:],
-                        lhsT=x_codes[:, g, t_cols].bitcast(FP8X4),
-                        lhsT_scale=x_scales[:, g, t_cols],
+                        lhsT=x_codes[:, half, g, t_cols].bitcast(FP8X4),
+                        lhsT_scale=x_scales[:, half, g, t_cols],
                         rhs=w_codes[:, g, :].bitcast(FP8X4),
                         rhs_scale=w_scales[:, g, :],
                         start=(g == 0),
                         stop=(g == PASSES - 1),
                     )
-                banks_of[unit].append(product)
+                banks_of[unit, i] = product
 
         def add_up(unit):
             e, j = divmod(unit, N_BLOCKS)
             n_cols = slice(N_BLOCK * j, N_BLOCK * (j + 1))
             for i in range(TOKEN_TILES):
-                nc.vector.scalar_tensor_tensor(
-                    out=total[:, i, n_cols],
-                    in0=banks_of[unit][i][:],
-                    scalar=gate[:, i, e : e + 1],
-                    in1=total[:, i, n_cols],
-                    op0=ALU.mult,
-                    op1=ALU.add,
-                )
+                if e == 0:
+                    nc.scalar.activation(
+                        out=total[:, i, n_cols], in_=banks_of[unit, i][:], func=ACT.Copy, scale=gate[:, i, 0:1]
+                    )
+                else:
+                    nc.vector.scalar_tensor_tensor(
+                        out=total[:, i, n_cols],
+                        in0=banks_of[unit, i][:],
+                        scalar=gate[:, i, e : e + 1],
+                        in1=total[:, i, n_cols],
+                        op0=ALU.mult,
+                        op1=ALU.add,
+                    )
                 if e == E - 1:
                     nc.sync.dma_start(out=out_rows[:, i, n_cols], in_=total[:, i, n_cols])
 
-        regroup(0)
-
-        gate_t_bank = psum.tile([P, TOKEN_TILES, P], BF16, tag="bank")
-        for i in range(TOKEN_TILES):
-            nc.tensor.transpose(gate_t_bank[:, i, :], gate_parts[:, i, :], identity_bf16[:])
         gate_t = keep.tile([P, TOKEN_TILES, P], BF16)
-        nc.vector.tensor_copy(out=gate_t[:], in_=gate_t_bank[:])
-        for j in range(N_BLOCKS):
-            n_cols = slice(N_BLOCK * j, N_BLOCK * (j + 1))
-            for i in range(TOKEN_TILES):
-                bias_bank = psum.tile([P, N_BLOCK], F32, tag="bank")
-                nc.tensor.matmul(bias_bank[:], lhsT=gate_t[:, i, :], rhs=be_rows[:, n_cols], start=True, stop=True)
-                copy = nc.vector.tensor_copy if i % 2 == 0 else nc.scalar.copy
-                copy(out=total[:, i, n_cols], in_=bias_bank[:])
 
-        for unit in range(UNITS):
+        def split_gate():
+            rest = gate
+            for part in range(GATE_PARTS):
+                kept = gate_parts[:, :, E * part : E * (part + 1)]
+                nc.vector.tensor_copy(out=kept, in_=rest[:])
+                if part < GATE_PARTS - 1:
+                    smaller = keep.tile([P, TOKEN_TILES, E], F32, name="rest%d" % part)
+                    nc.vector.tensor_tensor(out=smaller[:], in0=rest[:], in1=kept, op=ALU.subtract)
+                    rest = smaller
+
+        def turn_gate():
+            bank = psum.tile([P, TOKEN_TILES, P], BF16, tag="bank")
+            for i in range(TOKEN_TILES):
+                nc.tensor.transpose(bank[:, i, :], gate_parts[:, i, :], identity_bf16[:])
+            return bank
+
+        def multiply_bias(i, j):
+            bias_bank = psum.tile([P, N_BLOCK], F32, tag="bank")
+            n_cols = slice(N_BLOCK * j, N_BLOCK * (j + 1))
+            nc.tensor.matmul(bias_bank[:], lhsT=gate_t[:, i, :], rhs=be_rows[:, n_cols], start=True, stop=True)
+            return bias_bank
+
+        def add_bias(bias_bank, i, j):
+            n_cols = slice(N_BLOCK * j, N_BLOCK * (j + 1))
+            nc.vector.tensor_tensor(out=total[:, i, n_cols], in0=bias_bank[:], in1=total[:, i, n_cols], op=ALU.add)
+
+        x_banks = turn_x(0)
+        split_gate()
+        gate_t_bank = turn_gate()
+        group_x(0, x_banks)
+        regroup(0)
+        x_banks = turn_x(1)
+        regroup_on_vector(0)
+        quantize_x(0)
+        codes = quantize(0)
+        group_x(1, x_banks)
+        nc.scalar.copy(out=gate_t[:], in_=gate_t_bank[:])
+        multiply(0, *codes, tiles=range(2))
+        regroup(1)
+        regroup_on_tensor(1)
+        regroup_on_vector(1)
+        quantize_x(1)
+        multiply(0, *codes, tiles=range(2, 4))
+        regroup(2)
+        regroup_on_tensor(2)
+        add_up(0)
+
+        for unit in range(1, UNITS):
+            codes = quantize(unit)
+            bias_block = divmod(unit - BIAS_UNIT, N_BLOCKS) if 0 <= unit - BIAS_UNIT < N_BLOCKS * TOKEN_TILES else None
+            if bias_block:
+                bias_bank = multiply_bias(*bias_block)
+            multiply(unit, *codes)
+            if unit < N_BLOCKS:
+                add_up(unit)
+            if unit + 2 < UNITS:
+                load(unit + 2)
+                regroup(unit + 2)
+                regroup_on_tensor(unit + 2)
             if unit + 1 < UNITS:
-                regroup(unit + 1)
-            multiply(unit)
-            if unit >= 1:
+                regroup_on_vector(unit + 1)
+            if unit - 1 >= N_BLOCKS:
                 add_up(unit - 1)
+            if bias_block:
+                add_bias(bias_bank, *bias_block)
         add_up(UNITS - 1)

@@ -41,7 +41,7 @@ def tile_enhancedmathematicalreasoning_pa_kernel(tc, hidden_states, op_logits, W
     logit_rows = op_logits.flatten_outer_dims().rearrange("(p i) e -> p i e", i=TOKEN_TILES)
     out_rows = out.flatten_outer_dims().rearrange("(p i) n -> p i n", i=TOKEN_TILES)
 
-    with tc.tile_pool(name="keep", bufs=1) as keep, tc.tile_pool(name="w_in", bufs=6) as w_in, tc.tile_pool(
+    with tc.tile_pool(name="keep", bufs=1) as keep, tc.tile_pool(name="w_in", bufs=8) as w_in, tc.tile_pool(
         name="w_mx", bufs=4
     ) as w_mx, tc.psum_pool(name="psum", bufs=8) as psum, tc.manual_schedule():
         x_raw = keep.tile([P, TOKEN_TILES, H], BF16)
@@ -53,25 +53,26 @@ def tile_enhancedmathematicalreasoning_pa_kernel(tc, hidden_states, op_logits, W
             tiles = slice(2 * half, 2 * half + 2)
             nc.sync.dma_start(out=x_raw[:, tiles, :], in_=x_rows[:, tiles, :])
 
-        def load(unit):
-            e, j = divmod(unit, N_BLOCKS)
-            w_raw = w_in.tile([P, PASSES, PACK, N_BLOCK], BF16)
+        def load(e, n_cols=slice(0, HO)):
             for g in range(PASSES):
+                if (e, g) not in raw_of:
+                    raw_of[e, g] = w_in.tile([P, PACK, HO], BF16, name="w_raw")
                 nc.sync.dma_start(
-                    out=w_raw[:, g],
-                    in_=We[e, K_PASS * g : K_PASS * (g + 1), N_BLOCK * j : N_BLOCK * (j + 1)].rearrange(
-                        "(p t) n -> p t n", t=PACK
-                    ),
+                    out=raw_of[e, g][:, :, n_cols],
+                    in_=We[e, K_PASS * g : K_PASS * (g + 1), n_cols].rearrange("(p t) n -> p t n", t=PACK),
                 )
-            raw_of[unit] = w_raw
+
+        def raw(unit, g, cols):
+            e, j = divmod(unit, N_BLOCKS)
+            return raw_of[e, g][:, :, N_BLOCK * j + cols.start : N_BLOCK * j + cols.stop]
 
         logits = keep.tile([P, TOKEN_TILES, E], BF16)
         nc.sync.dma_start(out=logits[:], in_=logit_rows)
         load_x(0)
-        load(0)
+        load(0, slice(0, N_BLOCK))
         load_x(1)
+        load(0, slice(N_BLOCK, HO))
         load(1)
-        load(2)
         identity_f32 = keep.tile([P, P], F32)
         make_identity(nc, identity_f32[:])
         identity_bf16 = keep.tile([P, P], BF16)
@@ -152,17 +153,17 @@ def tile_enhancedmathematicalreasoning_pa_kernel(tc, hidden_states, op_logits, W
             for g in range(PASSES) if cols.stop > cols.start else ():
                 copy(
                     out=grouped_of[unit][:, g, cols, :].rearrange("p (c i) t -> p c t i", i=RUN),
-                    in_=raw_of[unit][:, g, :, cols].rearrange("p t (c i) -> p c t i", i=RUN),
+                    in_=raw(unit, g, cols).rearrange("p t (c i) -> p c t i", i=RUN),
                 )
 
         def regroup(unit):
             grouped_of[unit] = w_mx.tile([P, PASSES, N_BLOCK, PACK], BF16, align_bytes=64, name="w_grouped")
             helper_start = N_BLOCK - helper_cols(unit)
             copy_cols(nc.scalar.copy, unit, slice(tensor_cols(unit) + vector_cols(unit), helper_start))
-            for passes in (slice(0, 1), slice(1, 2)) if unit < HEAD_UNITS else (slice(0, 2),):
+            for g in range(PASSES):
                 nc.gpsimd.tensor_scalar(
-                    out=grouped_of[unit][:, passes, helper_start:, :],
-                    in0=raw_of[unit][:, passes, :, helper_start:].rearrange("p g t n -> p g n t"),
+                    out=grouped_of[unit][:, g, helper_start:, :],
+                    in0=raw(unit, g, slice(helper_start, N_BLOCK)).rearrange("p t n -> p n t"),
                     scalar1=1.0,
                     scalar2=0.0,
                     op0=ALU.mult,
@@ -175,7 +176,7 @@ def tile_enhancedmathematicalreasoning_pa_kernel(tc, hidden_states, op_logits, W
                 nc.tensor.matmul(
                     bank[:, g, :],
                     lhsT=identity_bf16[:],
-                    rhs=raw_of[unit][:, g, :, :TENSOR_COLS].rearrange("p t n -> p n t"),
+                    rhs=raw(unit, g, slice(0, TENSOR_COLS)).rearrange("p t n -> p n t"),
                     start=True,
                     stop=True,
                 )
@@ -284,6 +285,9 @@ def tile_enhancedmathematicalreasoning_pa_kernel(tc, hidden_states, op_logits, W
         add_up(0)
 
         for unit in range(1, UNITS):
+            e, j = divmod(unit, N_BLOCKS)
+            if j == 1 and e + 2 < E:
+                load(e + 2)
             codes = quantize(unit)
             bias_block = divmod(unit - BIAS_UNIT, N_BLOCKS) if 0 <= unit - BIAS_UNIT < N_BLOCKS * TOKEN_TILES else None
             if bias_block:
@@ -292,7 +296,6 @@ def tile_enhancedmathematicalreasoning_pa_kernel(tc, hidden_states, op_logits, W
             if unit < N_BLOCKS:
                 add_up(unit)
             if unit + 2 < UNITS:
-                load(unit + 2)
                 regroup(unit + 2)
                 regroup_on_tensor(unit + 2)
             if unit + 1 < UNITS:

@@ -23,13 +23,8 @@ N_BLOCK = 512
 N_BLOCKS = HO // N_BLOCK
 UNITS = E * N_BLOCKS
 RUN = 4
-HELPER_COLS = 128
-TENSOR_COLS = 128
-HEAD_UNITS = 4
-HEAD_VECTOR_COLS = 288
-HEAD_HELPER_COLS = 96
-FIRST_VECTOR_COLS = 320
-BIAS_UNIT = 4
+HELPER_COLS = 160
+HEAD_COLS = ((320, 160), (192, 256), (0, 256))
 GATE_PARTS = 3
 
 FLOPS = 2 * TOKENS * H * HO * E
@@ -53,36 +48,46 @@ def tile_enhancedmathematicalreasoning_pa_kernel(tc, hidden_states, op_logits, W
             tiles = slice(2 * half, 2 * half + 2)
             nc.sync.dma_start(out=x_raw[:, tiles, :], in_=x_rows[:, tiles, :])
 
-        def load(e, n_cols=slice(0, HO)):
+        def load_first(unit):
+            raw_of[unit] = []
             for g in range(PASSES):
-                if (e, g) not in raw_of:
-                    raw_of[e, g] = w_in.tile([P, PACK, HO], BF16, name="w_raw")
+                w_raw = keep.tile([P, PACK, N_BLOCK], BF16, name="w_first_%d_%d" % (unit, g))
                 nc.sync.dma_start(
-                    out=raw_of[e, g][:, :, n_cols],
-                    in_=We[e, K_PASS * g : K_PASS * (g + 1), n_cols].rearrange("(p t) n -> p t n", t=PACK),
+                    out=w_raw[:],
+                    in_=We[0, K_PASS * g : K_PASS * (g + 1), N_BLOCK * unit : N_BLOCK * (unit + 1)].rearrange(
+                        "(p t) n -> p t n", t=PACK
+                    ),
                 )
+                raw_of[unit].append(w_raw)
 
-        def raw(unit, g, cols):
-            e, j = divmod(unit, N_BLOCKS)
-            return raw_of[e, g][:, :, N_BLOCK * j + cols.start : N_BLOCK * j + cols.stop]
+        def load(e):
+            raw_of[N_BLOCKS * e], raw_of[N_BLOCKS * e + 1] = [], []
+            for g in range(PASSES):
+                w_raw = w_in.tile([P, PACK, HO], BF16)
+                nc.sync.dma_start(
+                    out=w_raw[:], in_=We[e, K_PASS * g : K_PASS * (g + 1), :].rearrange("(p t) n -> p t n", t=PACK)
+                )
+                for j in range(N_BLOCKS):
+                    raw_of[N_BLOCKS * e + j].append(w_raw[:, :, N_BLOCK * j : N_BLOCK * (j + 1)])
 
         logits = keep.tile([P, TOKEN_TILES, E], BF16)
         nc.sync.dma_start(out=logits[:], in_=logit_rows)
         load_x(0)
-        load(0, slice(0, N_BLOCK))
+        load_first(0)
+        be_rows = keep.tile([P, HO], BF16)
+        nc.vector.memset(be_rows[:], 0.0)
+        for part in range(GATE_PARTS):
+            nc.sync.dma_start(out=be_rows[E * part : E * (part + 1), :], in_=be)
         load_x(1)
-        load(0, slice(N_BLOCK, HO))
-        load(1)
+        load_first(1)
+        for e in range(1, 5):
+            load(e)
         identity_f32 = keep.tile([P, P], F32)
         make_identity(nc, identity_f32[:])
         identity_bf16 = keep.tile([P, P], BF16)
         make_identity(nc, identity_bf16[:])
-        be_rows = keep.tile([P, HO], BF16)
-        nc.gpsimd.memset(be_rows[:], 0.0)
         gate_parts = keep.tile([P, TOKEN_TILES, P], BF16)
         nc.gpsimd.memset(gate_parts[:], 0.0)
-        for part in range(GATE_PARTS):
-            nc.sync.dma_start(out=be_rows[E * part : E * (part + 1), :], in_=be)
 
         row_max = keep.tile([P, TOKEN_TILES], F32)
         nc.vector.tensor_reduce(out=row_max[:], in_=logits[:], axis=AXIS.X, op=ALU.max)
@@ -138,56 +143,32 @@ def tile_enhancedmathematicalreasoning_pa_kernel(tc, hidden_states, op_logits, W
 
         total = keep.tile([P, TOKEN_TILES, HO], F32)
 
-        def tensor_cols(unit):
-            return TENSOR_COLS if unit > 0 else 0
+        def shares(unit):
+            return HEAD_COLS[unit] if unit < len(HEAD_COLS) else (0, HELPER_COLS)
 
-        def vector_cols(unit):
-            if unit == 0:
-                return FIRST_VECTOR_COLS
-            return HEAD_VECTOR_COLS if unit < HEAD_UNITS else 0
-
-        def helper_cols(unit):
-            return HEAD_HELPER_COLS if unit < HEAD_UNITS else HELPER_COLS
-
-        def copy_cols(copy, unit, cols):
-            for g in range(PASSES) if cols.stop > cols.start else ():
-                copy(
-                    out=grouped_of[unit][:, g, cols, :].rearrange("p (c i) t -> p c t i", i=RUN),
-                    in_=raw(unit, g, cols).rearrange("p t (c i) -> p c t i", i=RUN),
-                )
+        def copy_cols(copy, unit, g, cols):
+            copy(
+                out=grouped_of[unit][:, g, cols, :].rearrange("p (c i) t -> p c t i", i=RUN),
+                in_=raw_of[unit][g][:, :, cols].rearrange("p t (c i) -> p c t i", i=RUN),
+            )
 
         def regroup(unit):
             grouped_of[unit] = w_mx.tile([P, PASSES, N_BLOCK, PACK], BF16, align_bytes=64, name="w_grouped")
-            helper_start = N_BLOCK - helper_cols(unit)
-            copy_cols(nc.scalar.copy, unit, slice(tensor_cols(unit) + vector_cols(unit), helper_start))
+            vector_cols, helper_cols = shares(unit)
+            helper_start = N_BLOCK - helper_cols
             for g in range(PASSES):
+                copy_cols(nc.scalar.copy, unit, g, slice(vector_cols, helper_start))
                 nc.gpsimd.tensor_scalar(
                     out=grouped_of[unit][:, g, helper_start:, :],
-                    in0=raw(unit, g, slice(helper_start, N_BLOCK)).rearrange("p t n -> p n t"),
+                    in0=raw_of[unit][g][:, :, helper_start:].rearrange("p t n -> p n t"),
                     scalar1=1.0,
                     scalar2=0.0,
                     op0=ALU.mult,
                     op1=ALU.add,
                 )
 
-        def regroup_on_tensor(unit):
-            bank = psum.tile([P, PASSES, TENSOR_COLS * PACK], BF16, tag="bank")
-            for g in range(PASSES):
-                nc.tensor.matmul(
-                    bank[:, g, :],
-                    lhsT=identity_bf16[:],
-                    rhs=raw(unit, g, slice(0, TENSOR_COLS)).rearrange("p t n -> p n t"),
-                    start=True,
-                    stop=True,
-                )
-            for g in range(PASSES):
-                nc.scalar.copy(
-                    out=grouped_of[unit][:, g, :TENSOR_COLS, :].rearrange("p n t -> p (n t)"), in_=bank[:, g, :]
-                )
-
-        def regroup_on_vector(unit):
-            start = tensor_cols(unit)
-            copy_cols(nc.vector.tensor_copy, unit, slice(start, start + vector_cols(unit)))
+        def regroup_on_vector(unit, g):
+            copy_cols(nc.vector.tensor_copy, unit, g, slice(0, shares(unit)[0]))
 
         def quantize(unit):
             w_codes = w_mx.tile([P, PASSES, N_BLOCK], U32, align_bytes=64)
@@ -215,23 +196,18 @@ def tile_enhancedmathematicalreasoning_pa_kernel(tc, hidden_states, op_logits, W
                     )
                 banks_of[unit, i] = product
 
-        def add_up(unit):
+        def add_up(unit, tiles=range(TOKEN_TILES)):
             e, j = divmod(unit, N_BLOCKS)
             n_cols = slice(N_BLOCK * j, N_BLOCK * (j + 1))
-            for i in range(TOKEN_TILES):
-                if e == 0:
-                    nc.scalar.activation(
-                        out=total[:, i, n_cols], in_=banks_of[unit, i][:], func=ACT.Copy, scale=gate[:, i, 0:1]
-                    )
-                else:
-                    nc.vector.scalar_tensor_tensor(
-                        out=total[:, i, n_cols],
-                        in0=banks_of[unit, i][:],
-                        scalar=gate[:, i, e : e + 1],
-                        in1=total[:, i, n_cols],
-                        op0=ALU.mult,
-                        op1=ALU.add,
-                    )
+            for i in tiles:
+                nc.vector.scalar_tensor_tensor(
+                    out=total[:, i, n_cols],
+                    in0=banks_of[unit, i][:],
+                    scalar=gate[:, i, e : e + 1],
+                    in1=total[:, i, n_cols],
+                    op0=ALU.mult,
+                    op1=ALU.add,
+                )
                 if e == E - 1:
                     nc.sync.dma_start(out=out_rows[:, i, n_cols], in_=total[:, i, n_cols])
 
@@ -253,55 +229,51 @@ def tile_enhancedmathematicalreasoning_pa_kernel(tc, hidden_states, op_logits, W
                 nc.tensor.transpose(bank[:, i, :], gate_parts[:, i, :], identity_bf16[:])
             return bank
 
-        def multiply_bias(i, j):
-            bias_bank = psum.tile([P, N_BLOCK], F32, tag="bank")
+        def multiply_bias(j):
             n_cols = slice(N_BLOCK * j, N_BLOCK * (j + 1))
-            nc.tensor.matmul(bias_bank[:], lhsT=gate_t[:, i, :], rhs=be_rows[:, n_cols], start=True, stop=True)
-            return bias_bank
+            bias_banks = []
+            for i in range(TOKEN_TILES):
+                bias_bank = psum.tile([P, N_BLOCK], F32, tag="bank")
+                nc.tensor.matmul(bias_bank[:], lhsT=gate_t[:, i, :], rhs=be_rows[:, n_cols], start=True, stop=True)
+                bias_banks.append(bias_bank)
+            return bias_banks
 
-        def add_bias(bias_bank, i, j):
+        def start_sum(j, bias_banks):
             n_cols = slice(N_BLOCK * j, N_BLOCK * (j + 1))
-            nc.vector.tensor_tensor(out=total[:, i, n_cols], in0=bias_bank[:], in1=total[:, i, n_cols], op=ALU.add)
+            for i in range(TOKEN_TILES):
+                nc.scalar.copy(out=total[:, i, n_cols], in_=bias_banks[i][:])
 
         x_banks = turn_x(0)
         split_gate()
         gate_t_bank = turn_gate()
         group_x(0, x_banks)
+        nc.vector.tensor_copy(out=gate_t[:], in_=gate_t_bank[:])
         regroup(0)
-        x_banks = turn_x(1)
-        regroup_on_vector(0)
+        regroup_on_vector(0, 0)
         quantize_x(0)
+        regroup_on_vector(0, 1)
+        bias_banks = multiply_bias(0)
+        start_sum(0, bias_banks)
         codes = quantize(0)
+        x_banks = turn_x(1)
         group_x(1, x_banks)
-        nc.scalar.copy(out=gate_t[:], in_=gate_t_bank[:])
+        bias_banks = multiply_bias(1)
         multiply(0, *codes, tiles=range(2))
         regroup(1)
-        regroup_on_tensor(1)
-        regroup_on_vector(1)
+        for g in range(PASSES):
+            regroup_on_vector(1, g)
         quantize_x(1)
         multiply(0, *codes, tiles=range(2, 4))
-        regroup(2)
-        regroup_on_tensor(2)
-        add_up(0)
+        start_sum(1, bias_banks)
+        add_up(0, tiles=range(2))
 
         for unit in range(1, UNITS):
-            e, j = divmod(unit, N_BLOCKS)
-            if j == 1 and e + 2 < E:
-                load(e + 2)
             codes = quantize(unit)
-            bias_block = divmod(unit - BIAS_UNIT, N_BLOCKS) if 0 <= unit - BIAS_UNIT < N_BLOCKS * TOKEN_TILES else None
-            if bias_block:
-                bias_bank = multiply_bias(*bias_block)
-            multiply(unit, *codes)
-            if unit < N_BLOCKS:
-                add_up(unit)
-            if unit + 2 < UNITS:
-                regroup(unit + 2)
-                regroup_on_tensor(unit + 2)
             if unit + 1 < UNITS:
-                regroup_on_vector(unit + 1)
-            if unit - 1 >= N_BLOCKS:
-                add_up(unit - 1)
-            if bias_block:
-                add_bias(bias_bank, *bias_block)
+                regroup(unit + 1)
+            e, j = divmod(unit + 1, N_BLOCKS)
+            if j == 1 and 5 <= e + 4 < E:
+                load(e + 4)
+            multiply(unit, *codes)
+            add_up(unit - 1, tiles=range(2, 4) if unit == 1 else range(TOKEN_TILES))
         add_up(UNITS - 1)

@@ -24,7 +24,7 @@ N_BLOCKS = HO // N_BLOCK
 UNITS = E * N_BLOCKS
 RUN = 4
 HELPER_COLS = 160
-HEAD_COLS = ((320, 160), (192, 256), (0, 256))
+HEAD_COLS = ((320, 0), (256, 64), (192, 64), (192, 64), (128, 64))
 GATE_PARTS = 3
 
 FLOPS = 2 * TOKENS * H * HO * E
@@ -36,8 +36,8 @@ def tile_enhancedmathematicalreasoning_pa_kernel(tc, hidden_states, op_logits, W
     logit_rows = op_logits.flatten_outer_dims().rearrange("(p i) e -> p i e", i=TOKEN_TILES)
     out_rows = out.flatten_outer_dims().rearrange("(p i) n -> p i n", i=TOKEN_TILES)
 
-    with tc.tile_pool(name="keep", bufs=1) as keep, tc.tile_pool(name="w_in", bufs=8) as w_in, tc.tile_pool(
-        name="w_mx", bufs=4
+    with tc.tile_pool(name="keep", bufs=1) as keep, tc.tile_pool(name="w_in", bufs=6) as w_in, tc.tile_pool(
+        name="w_mx", bufs=2
     ) as w_mx, tc.psum_pool(name="psum", bufs=8) as psum, tc.manual_schedule():
         x_raw = keep.tile([P, TOKEN_TILES, H], BF16)
         raw_of = {}
@@ -48,40 +48,28 @@ def tile_enhancedmathematicalreasoning_pa_kernel(tc, hidden_states, op_logits, W
             tiles = slice(2 * half, 2 * half + 2)
             nc.sync.dma_start(out=x_raw[:, tiles, :], in_=x_rows[:, tiles, :])
 
-        def load_first(unit):
-            raw_of[unit] = []
+        def load(unit):
+            e, j = divmod(unit, N_BLOCKS)
+            raw_of[unit] = w_in.tile([P, PASSES, PACK, N_BLOCK], BF16, name="w_raw")
             for g in range(PASSES):
-                w_raw = keep.tile([P, PACK, N_BLOCK], BF16, name="w_first_%d_%d" % (unit, g))
                 nc.sync.dma_start(
-                    out=w_raw[:],
-                    in_=We[0, K_PASS * g : K_PASS * (g + 1), N_BLOCK * unit : N_BLOCK * (unit + 1)].rearrange(
+                    out=raw_of[unit][:, g],
+                    in_=We[e, K_PASS * g : K_PASS * (g + 1), N_BLOCK * j : N_BLOCK * (j + 1)].rearrange(
                         "(p t) n -> p t n", t=PACK
                     ),
                 )
-                raw_of[unit].append(w_raw)
-
-        def load(e):
-            raw_of[N_BLOCKS * e], raw_of[N_BLOCKS * e + 1] = [], []
-            for g in range(PASSES):
-                w_raw = w_in.tile([P, PACK, HO], BF16)
-                nc.sync.dma_start(
-                    out=w_raw[:], in_=We[e, K_PASS * g : K_PASS * (g + 1), :].rearrange("(p t) n -> p t n", t=PACK)
-                )
-                for j in range(N_BLOCKS):
-                    raw_of[N_BLOCKS * e + j].append(w_raw[:, :, N_BLOCK * j : N_BLOCK * (j + 1)])
 
         logits = keep.tile([P, TOKEN_TILES, E], BF16)
         nc.sync.dma_start(out=logits[:], in_=logit_rows)
         load_x(0)
-        load_first(0)
+        load(0)
         be_rows = keep.tile([P, HO], BF16)
         nc.vector.memset(be_rows[:], 0.0)
         for part in range(GATE_PARTS):
             nc.sync.dma_start(out=be_rows[E * part : E * (part + 1), :], in_=be)
         load_x(1)
-        load_first(1)
-        for e in range(1, 5):
-            load(e)
+        load(1)
+        load(2)
         identity_f32 = keep.tile([P, P], F32)
         make_identity(nc, identity_f32[:])
         identity_bf16 = keep.tile([P, P], BF16)
@@ -149,7 +137,7 @@ def tile_enhancedmathematicalreasoning_pa_kernel(tc, hidden_states, op_logits, W
         def copy_cols(copy, unit, g, cols):
             copy(
                 out=grouped_of[unit][:, g, cols, :].rearrange("p (c i) t -> p c t i", i=RUN),
-                in_=raw_of[unit][g][:, :, cols].rearrange("p t (c i) -> p c t i", i=RUN),
+                in_=raw_of[unit][:, g, :, cols].rearrange("p t (c i) -> p c t i", i=RUN),
             )
 
         def regroup(unit):
@@ -158,9 +146,10 @@ def tile_enhancedmathematicalreasoning_pa_kernel(tc, hidden_states, op_logits, W
             helper_start = N_BLOCK - helper_cols
             for g in range(PASSES):
                 copy_cols(nc.scalar.copy, unit, g, slice(vector_cols, helper_start))
+            if helper_cols:
                 nc.gpsimd.tensor_scalar(
-                    out=grouped_of[unit][:, g, helper_start:, :],
-                    in0=raw_of[unit][g][:, :, helper_start:].rearrange("p t n -> p n t"),
+                    out=grouped_of[unit][:, :, helper_start:, :],
+                    in0=raw_of[unit][:, :, :, helper_start:].rearrange("p g t n -> p g n t"),
                     scalar1=1.0,
                     scalar2=0.0,
                     op0=ALU.mult,
@@ -168,7 +157,8 @@ def tile_enhancedmathematicalreasoning_pa_kernel(tc, hidden_states, op_logits, W
                 )
 
         def regroup_on_vector(unit, g):
-            copy_cols(nc.vector.tensor_copy, unit, g, slice(0, shares(unit)[0]))
+            if shares(unit)[0]:
+                copy_cols(nc.vector.tensor_copy, unit, g, slice(0, shares(unit)[0]))
 
         def quantize(unit):
             w_codes = w_mx.tile([P, PASSES, N_BLOCK], U32, align_bytes=64)
@@ -257,23 +247,26 @@ def tile_enhancedmathematicalreasoning_pa_kernel(tc, hidden_states, op_logits, W
         codes = quantize(0)
         x_banks = turn_x(1)
         group_x(1, x_banks)
-        bias_banks = multiply_bias(1)
         multiply(0, *codes, tiles=range(2))
         regroup(1)
         for g in range(PASSES):
             regroup_on_vector(1, g)
         quantize_x(1)
+        bias_banks = multiply_bias(1)
         multiply(0, *codes, tiles=range(2, 4))
-        start_sum(1, bias_banks)
         add_up(0, tiles=range(2))
 
         for unit in range(1, UNITS):
             codes = quantize(unit)
             if unit + 1 < UNITS:
                 regroup(unit + 1)
-            e, j = divmod(unit + 1, N_BLOCKS)
-            if j == 1 and 5 <= e + 4 < E:
-                load(e + 4)
+                if unit + 1 < len(HEAD_COLS):
+                    for g in range(PASSES):
+                        regroup_on_vector(unit + 1, g)
+            if unit == 1:
+                start_sum(1, bias_banks)
+            if unit + 2 < UNITS:
+                load(unit + 2)
             multiply(unit, *codes)
             add_up(unit - 1, tiles=range(2, 4) if unit == 1 else range(TOKEN_TILES))
         add_up(UNITS - 1)

@@ -21,10 +21,13 @@ PASSES = H // K_PASS
 TOKEN_TILES = TOKENS // P
 N_BLOCK = 512
 N_BLOCKS = HO // N_BLOCK
-UNITS = E * N_BLOCKS
+UNITS = N_BLOCKS * E
 RUN = 4
-HELPER_COLS = 160
-HEAD_COLS = ((320, 0), (256, 64), (192, 64), (192, 64), (128, 64))
+HELPER_COLS = 128
+HEAD_COLS = ((256, 0), (192, 64), (128, 64), (64, 96))
+BIAS_UNITS = (2, 4, 6, 8)
+TAIL_TILE = 3
+TAIL_UNITS = (UNITS - 2, UNITS - 1)
 GATE_PARTS = 3
 
 FLOPS = 2 * TOKENS * H * HO * E
@@ -43,13 +46,15 @@ def tile_enhancedmathematicalreasoning_pa_kernel(tc, hidden_states, op_logits, W
         raw_of = {}
         grouped_of = {}
         banks_of = {}
+        codes_of = {}
+        last_word = keep.tile([P, 1], U32)
 
         def load_x(half):
             tiles = slice(2 * half, 2 * half + 2)
             nc.sync.dma_start(out=x_raw[:, tiles, :], in_=x_rows[:, tiles, :])
 
         def load(unit):
-            e, j = divmod(unit, N_BLOCKS)
+            j, e = divmod(unit, E)
             raw_of[unit] = w_in.tile([P, PASSES, PACK, N_BLOCK], BF16, name="w_raw")
             for g in range(PASSES):
                 nc.sync.dma_start(
@@ -68,8 +73,8 @@ def tile_enhancedmathematicalreasoning_pa_kernel(tc, hidden_states, op_logits, W
         for part in range(GATE_PARTS):
             nc.sync.dma_start(out=be_rows[E * part : E * (part + 1), :], in_=be)
         load_x(1)
-        load(1)
-        load(2)
+        for unit in range(1, 5):
+            load(unit)
         identity_f32 = keep.tile([P, P], F32)
         make_identity(nc, identity_f32[:])
         identity_bf16 = keep.tile([P, P], BF16)
@@ -140,6 +145,9 @@ def tile_enhancedmathematicalreasoning_pa_kernel(tc, hidden_states, op_logits, W
                 in_=raw_of[unit][:, g, :, cols].rearrange("p t (c i) -> p c t i", i=RUN),
             )
 
+        def wait_for_quantize(unit):
+            nc.gpsimd.tensor_copy(out=last_word[:], in_=codes_of[unit][:, 0, 0:1])
+
         def regroup(unit):
             grouped_of[unit] = w_mx.tile([P, PASSES, N_BLOCK, PACK], BF16, align_bytes=64, name="w_grouped")
             vector_cols, helper_cols = shares(unit)
@@ -147,6 +155,8 @@ def tile_enhancedmathematicalreasoning_pa_kernel(tc, hidden_states, op_logits, W
             for g in range(PASSES):
                 copy_cols(nc.scalar.copy, unit, g, slice(vector_cols, helper_start))
             if helper_cols:
+                if unit > 0:
+                    wait_for_quantize(unit - 1)
                 nc.gpsimd.tensor_scalar(
                     out=grouped_of[unit][:, :, helper_start:, :],
                     in0=raw_of[unit][:, :, :, helper_start:].rearrange("p g t n -> p g n t"),
@@ -168,6 +178,7 @@ def tile_enhancedmathematicalreasoning_pa_kernel(tc, hidden_states, op_logits, W
                 scales=w_scales[:].rearrange("p g n -> p (g n)"),
                 in_=grouped_of[unit][:].rearrange("p g n t -> p (g n t)"),
             )
+            codes_of[unit] = w_codes
             return w_codes, w_scales
 
         def multiply(unit, w_codes, w_scales, tiles=range(TOKEN_TILES)):
@@ -187,18 +198,28 @@ def tile_enhancedmathematicalreasoning_pa_kernel(tc, hidden_states, op_logits, W
                 banks_of[unit, i] = product
 
         def add_up(unit, tiles=range(TOKEN_TILES)):
-            e, j = divmod(unit, N_BLOCKS)
+            j, e = divmod(unit, E)
             n_cols = slice(N_BLOCK * j, N_BLOCK * (j + 1))
             for i in tiles:
-                nc.vector.scalar_tensor_tensor(
-                    out=total[:, i, n_cols],
-                    in0=banks_of[unit, i][:],
-                    scalar=gate[:, i, e : e + 1],
-                    in1=total[:, i, n_cols],
-                    op0=ALU.mult,
-                    op1=ALU.add,
-                )
-                if e == E - 1:
+                if i == TAIL_TILE and unit in TAIL_UNITS:
+                    weighted = keep.tile([P, N_BLOCK], F32, name="weighted%d" % unit)
+                    nc.scalar.activation(
+                        out=weighted[:], in_=banks_of[unit, i][:], func=ACT.Copy, scale=gate[:, i, e : e + 1]
+                    )
+                    wait_for_quantize(UNITS - 1)
+                    nc.gpsimd.tensor_tensor(
+                        out=total[:, i, n_cols], in0=weighted[:], in1=total[:, i, n_cols], op=ALU.add
+                    )
+                else:
+                    nc.vector.scalar_tensor_tensor(
+                        out=total[:, i, n_cols],
+                        in0=banks_of[unit, i][:],
+                        scalar=gate[:, i, e : e + 1],
+                        in1=total[:, i, n_cols],
+                        op0=ALU.mult,
+                        op1=ALU.add,
+                    )
+                if e == E - 1 and not (i == TAIL_TILE and unit in TAIL_UNITS):
                     nc.sync.dma_start(out=out_rows[:, i, n_cols], in_=total[:, i, n_cols])
 
         gate_t = keep.tile([P, TOKEN_TILES, P], BF16)
@@ -219,19 +240,19 @@ def tile_enhancedmathematicalreasoning_pa_kernel(tc, hidden_states, op_logits, W
                 nc.tensor.transpose(bank[:, i, :], gate_parts[:, i, :], identity_bf16[:])
             return bank
 
-        def multiply_bias(j):
+        def multiply_bias(j, tiles=range(TOKEN_TILES)):
             n_cols = slice(N_BLOCK * j, N_BLOCK * (j + 1))
-            bias_banks = []
-            for i in range(TOKEN_TILES):
+            bias_banks = {}
+            for i in tiles:
                 bias_bank = psum.tile([P, N_BLOCK], F32, tag="bank")
                 nc.tensor.matmul(bias_bank[:], lhsT=gate_t[:, i, :], rhs=be_rows[:, n_cols], start=True, stop=True)
-                bias_banks.append(bias_bank)
+                bias_banks[i] = bias_bank
             return bias_banks
 
         def start_sum(j, bias_banks):
             n_cols = slice(N_BLOCK * j, N_BLOCK * (j + 1))
-            for i in range(TOKEN_TILES):
-                nc.scalar.copy(out=total[:, i, n_cols], in_=bias_banks[i][:])
+            for i, bank in bias_banks.items():
+                nc.scalar.copy(out=total[:, i, n_cols], in_=bank[:])
 
         x_banks = turn_x(0)
         split_gate()
@@ -252,21 +273,24 @@ def tile_enhancedmathematicalreasoning_pa_kernel(tc, hidden_states, op_logits, W
         for g in range(PASSES):
             regroup_on_vector(1, g)
         quantize_x(1)
-        bias_banks = multiply_bias(1)
         multiply(0, *codes, tiles=range(2, 4))
         add_up(0, tiles=range(2))
 
         for unit in range(1, UNITS):
             codes = quantize(unit)
+            if unit in BIAS_UNITS:
+                bias_banks = multiply_bias(1, tiles=(BIAS_UNITS.index(unit),))
             if unit + 1 < UNITS:
                 regroup(unit + 1)
                 if unit + 1 < len(HEAD_COLS):
                     for g in range(PASSES):
                         regroup_on_vector(unit + 1, g)
-            if unit == 1:
+            if unit + 4 < UNITS:
+                load(unit + 4)
+            if unit in BIAS_UNITS:
                 start_sum(1, bias_banks)
-            if unit + 2 < UNITS:
-                load(unit + 2)
-            multiply(unit, *codes)
+            multiply(unit, *codes, tiles=(3, 0, 1, 2) if unit == UNITS - 1 else range(TOKEN_TILES))
             add_up(unit - 1, tiles=range(2, 4) if unit == 1 else range(TOKEN_TILES))
-        add_up(UNITS - 1)
+        add_up(UNITS - 1, tiles=(3, 0, 1, 2))
+        n_cols = slice(N_BLOCK * (N_BLOCKS - 1), HO)
+        nc.sync.dma_start(out=out_rows[:, TAIL_TILE, n_cols], in_=total[:, TAIL_TILE, n_cols])

@@ -181,8 +181,11 @@ def tile_enhancedmathematicalreasoning_pa_kernel(tc, hidden_states, op_logits, W
             codes_of[unit] = w_codes
             return w_codes, w_scales
 
-        def multiply(unit, w_codes, w_scales, tiles=range(TOKEN_TILES)):
-            for i in tiles:
+        def tile_order(unit):
+            return range(TOKEN_TILES) if unit % 2 == 0 else range(TOKEN_TILES - 1, -1, -1)
+
+        def multiply(unit, w_codes, w_scales, tiles=None):
+            for i in tiles or tile_order(unit):
                 half, t_cols = i // 2, slice(P * (i % 2), P * (i % 2 + 1))
                 product = psum.tile([P, N_BLOCK], F32, tag="bank")
                 for g in range(PASSES):
@@ -197,10 +200,10 @@ def tile_enhancedmathematicalreasoning_pa_kernel(tc, hidden_states, op_logits, W
                     )
                 banks_of[unit, i] = product
 
-        def add_up(unit, tiles=range(TOKEN_TILES)):
+        def add_up(unit, tiles=None):
             j, e = divmod(unit, E)
             n_cols = slice(N_BLOCK * j, N_BLOCK * (j + 1))
-            for i in tiles:
+            for i in tiles or tile_order(unit):
                 if i == TAIL_TILE and unit in TAIL_UNITS:
                     weighted = keep.tile([P, N_BLOCK], F32, name="weighted%d" % unit)
                     nc.scalar.activation(
@@ -289,8 +292,8 @@ def tile_enhancedmathematicalreasoning_pa_kernel(tc, hidden_states, op_logits, W
                 load(unit + 4)
             if unit in BIAS_UNITS:
                 start_sum(1, bias_banks)
-            multiply(unit, *codes, tiles=(3, 0, 1, 2) if unit == UNITS - 1 else range(TOKEN_TILES))
-            add_up(unit - 1, tiles=range(2, 4) if unit == 1 else range(TOKEN_TILES))
-        add_up(UNITS - 1, tiles=(3, 0, 1, 2))
+            multiply(unit, *codes)
+            add_up(unit - 1, tiles=range(2, 4) if unit == 1 else None)
+        add_up(UNITS - 1)
         n_cols = slice(N_BLOCK * (N_BLOCKS - 1), HO)
         nc.sync.dma_start(out=out_rows[:, TAIL_TILE, n_cols], in_=total[:, TAIL_TILE, n_cols])

@@ -23,8 +23,9 @@ N_BLOCK = 512
 N_BLOCKS = HO // N_BLOCK
 UNITS = N_BLOCKS * E
 RUN = 4
-HELPER_COLS = 128
-HEAD_COLS = ((256, 0), (192, 64), (128, 64), (64, 96))
+HELPER_COLS = 288
+HEAD_COLS = ((512, 0), (448, 64), (256, 128), (64, 224))
+SCALAR_COLS = PASSES * N_BLOCK - HELPER_COLS
 BIAS_UNITS = (2, 4, 6, 8)
 TAIL_TILE = 3
 TAIL_UNITS = (UNITS - 2, UNITS - 1)
@@ -44,7 +45,6 @@ def tile_enhancedmathematicalreasoning_pa_kernel(tc, hidden_states, op_logits, W
     ) as w_mx, tc.psum_pool(name="psum", bufs=8) as psum, tc.manual_schedule():
         x_raw = keep.tile([P, TOKEN_TILES, H], BF16)
         raw_of = {}
-        grouped_of = {}
         banks_of = {}
         codes_of = {}
         last_word = keep.tile([P, 1], U32)
@@ -53,10 +53,11 @@ def tile_enhancedmathematicalreasoning_pa_kernel(tc, hidden_states, op_logits, W
             tiles = slice(2 * half, 2 * half + 2)
             nc.sync.dma_start(out=x_raw[:, tiles, :], in_=x_rows[:, tiles, :])
 
-        def load(unit):
+        def load(unit, passes=range(PASSES)):
             j, e = divmod(unit, E)
-            raw_of[unit] = w_in.tile([P, PASSES, PACK, N_BLOCK], BF16, name="w_raw")
-            for g in range(PASSES):
+            if unit not in raw_of:
+                raw_of[unit] = w_in.tile([P, PASSES, PACK, N_BLOCK], BF16, name="w_raw")
+            for g in passes:
                 nc.sync.dma_start(
                     out=raw_of[unit][:, g],
                     in_=We[e, K_PASS * g : K_PASS * (g + 1), N_BLOCK * j : N_BLOCK * (j + 1)].rearrange(
@@ -66,12 +67,13 @@ def tile_enhancedmathematicalreasoning_pa_kernel(tc, hidden_states, op_logits, W
 
         logits = keep.tile([P, TOKEN_TILES, E], BF16)
         nc.sync.dma_start(out=logits[:], in_=logit_rows)
-        load_x(0)
-        load(0)
+        load(0, passes=range(1))
         be_rows = keep.tile([P, HO], BF16)
         nc.vector.memset(be_rows[:], 0.0)
         for part in range(GATE_PARTS):
             nc.sync.dma_start(out=be_rows[E * part : E * (part + 1), :], in_=be)
+        load(0, passes=range(1, PASSES))
+        load_x(0)
         load_x(1)
         for unit in range(1, 5):
             load(unit)
@@ -134,41 +136,54 @@ def tile_enhancedmathematicalreasoning_pa_kernel(tc, hidden_states, op_logits, W
                 in_=x_grouped[:, half].rearrange("p g r t -> p (g r t)"),
             )
 
-        total = keep.tile([P, TOKEN_TILES, HO], F32)
-
-        def shares(unit):
-            return HEAD_COLS[unit] if unit < len(HEAD_COLS) else (0, HELPER_COLS)
-
-        def copy_cols(copy, unit, g, cols):
-            copy(
-                out=grouped_of[unit][:, g, cols, :].rearrange("p (c i) t -> p c t i", i=RUN),
-                in_=raw_of[unit][:, g, :, cols].rearrange("p t (c i) -> p c t i", i=RUN),
-            )
-
         def wait_for_quantize(unit):
             nc.gpsimd.tensor_copy(out=last_word[:], in_=codes_of[unit][:, 0, 0:1])
 
-        def regroup(unit):
-            grouped_of[unit] = w_mx.tile([P, PASSES, N_BLOCK, PACK], BF16, align_bytes=64, name="w_grouped")
-            vector_cols, helper_cols = shares(unit)
-            helper_start = N_BLOCK - helper_cols
+        total = keep.tile([P, TOKEN_TILES, HO], F32)
+
+        stage = keep.tile([P, SCALAR_COLS + PASSES * N_BLOCK, PACK], BF16, align_bytes=64)
+
+        def grouped(unit):
+            start = SCALAR_COLS * (unit % 2)
+            return stage[:, start : start + PASSES * N_BLOCK, :]
+
+        def shares(unit):
+            vector_cols, helper_cols = HEAD_COLS[unit] if unit < len(HEAD_COLS) else (0, HELPER_COLS)
+            cols = PASSES * N_BLOCK
+            ends = [cols, cols - helper_cols, cols - helper_cols - vector_cols, 0]
+            if unit % 2 == 1:
+                ends = [cols - end for end in ends]
+            return [(min(pair), max(pair)) for pair in zip(ends[2::-1], ends[:0:-1])]
+
+        def cut(share):
+            found = []
             for g in range(PASSES):
-                copy_cols(nc.scalar.copy, unit, g, slice(vector_cols, helper_start))
-            if helper_cols:
-                if unit > 0:
-                    wait_for_quantize(unit - 1)
+                start, end = max(share[0], N_BLOCK * g), min(share[1], N_BLOCK * (g + 1))
+                if start < end:
+                    found.append((g, slice(start - N_BLOCK * g, end - N_BLOCK * g), slice(start, end)))
+            return found
+
+        def copy_cols(copy, unit, share):
+            for g, cols, both_cols in cut(share):
+                copy(
+                    out=grouped(unit)[:, both_cols, :].rearrange("p (c i) t -> p c t i", i=RUN),
+                    in_=raw_of[unit][:, g, :, cols].rearrange("p t (c i) -> p c t i", i=RUN),
+                )
+
+        def regroup(unit):
+            copy_cols(nc.scalar.copy, unit, shares(unit)[0])
+            for g, cols, both_cols in cut(shares(unit)[2]):
                 nc.gpsimd.tensor_scalar(
-                    out=grouped_of[unit][:, :, helper_start:, :],
-                    in0=raw_of[unit][:, :, :, helper_start:].rearrange("p g t n -> p g n t"),
+                    out=grouped(unit)[:, both_cols, :],
+                    in0=raw_of[unit][:, g, :, cols].rearrange("p t n -> p n t"),
                     scalar1=1.0,
                     scalar2=0.0,
                     op0=ALU.mult,
                     op1=ALU.add,
                 )
 
-        def regroup_on_vector(unit, g):
-            if shares(unit)[0]:
-                copy_cols(nc.vector.tensor_copy, unit, g, slice(0, shares(unit)[0]))
+        def regroup_on_vector(unit):
+            copy_cols(nc.vector.tensor_copy, unit, shares(unit)[1])
 
         def quantize(unit):
             w_codes = w_mx.tile([P, PASSES, N_BLOCK], U32, align_bytes=64)
@@ -176,7 +191,7 @@ def tile_enhancedmathematicalreasoning_pa_kernel(tc, hidden_states, op_logits, W
             nc.vector.quantize_mx(
                 out=w_codes[:].rearrange("p g n -> p (g n)").bitcast(FP8X4),
                 scales=w_scales[:].rearrange("p g n -> p (g n)"),
-                in_=grouped_of[unit][:].rearrange("p g n t -> p (g n t)"),
+                in_=grouped(unit).rearrange("p n t -> p (n t)"),
             )
             codes_of[unit] = w_codes
             return w_codes, w_scales
@@ -257,24 +272,22 @@ def tile_enhancedmathematicalreasoning_pa_kernel(tc, hidden_states, op_logits, W
             for i, bank in bias_banks.items():
                 nc.scalar.copy(out=total[:, i, n_cols], in_=bank[:])
 
-        x_banks = turn_x(0)
         split_gate()
         gate_t_bank = turn_gate()
-        group_x(0, x_banks)
-        nc.vector.tensor_copy(out=gate_t[:], in_=gate_t_bank[:])
         regroup(0)
-        regroup_on_vector(0, 0)
-        quantize_x(0)
-        regroup_on_vector(0, 1)
+        nc.vector.tensor_copy(out=gate_t[:], in_=gate_t_bank[:])
+        regroup_on_vector(0)
         bias_banks = multiply_bias(0)
         start_sum(0, bias_banks)
         codes = quantize(0)
+        x_banks = turn_x(0)
+        group_x(0, x_banks)
         x_banks = turn_x(1)
+        quantize_x(0)
         group_x(1, x_banks)
         multiply(0, *codes, tiles=range(2))
         regroup(1)
-        for g in range(PASSES):
-            regroup_on_vector(1, g)
+        regroup_on_vector(1)
         quantize_x(1)
         multiply(0, *codes, tiles=range(2, 4))
         add_up(0, tiles=range(2))
@@ -285,9 +298,7 @@ def tile_enhancedmathematicalreasoning_pa_kernel(tc, hidden_states, op_logits, W
                 bias_banks = multiply_bias(1, tiles=(BIAS_UNITS.index(unit),))
             if unit + 1 < UNITS:
                 regroup(unit + 1)
-                if unit + 1 < len(HEAD_COLS):
-                    for g in range(PASSES):
-                        regroup_on_vector(unit + 1, g)
+                regroup_on_vector(unit + 1)
             if unit + 4 < UNITS:
                 load(unit + 4)
             if unit in BIAS_UNITS:

@@ -23,8 +23,9 @@ N_BLOCK = 512
 N_BLOCKS = HO // N_BLOCK
 UNITS = N_BLOCKS * E
 RUN = 4
-HELPER_COLS = 288
-HEAD_COLS = ((512, 0), (448, 64), (256, 128), (64, 224))
+HELPER_COLS = 256
+HEAD_COLS = ((512, 0), (448, 64), (256, 128))
+BLOCK_0_VECTOR_COLS = 32
 SCALAR_COLS = PASSES * N_BLOCK - HELPER_COLS
 BIAS_UNITS = (2, 4, 6, 8)
 TAIL_TILE = 3
@@ -53,11 +54,10 @@ def tile_enhancedmathematicalreasoning_pa_kernel(tc, hidden_states, op_logits, W
             tiles = slice(2 * half, 2 * half + 2)
             nc.sync.dma_start(out=x_raw[:, tiles, :], in_=x_rows[:, tiles, :])
 
-        def load(unit, passes=range(PASSES)):
+        def load(unit):
             j, e = divmod(unit, E)
-            if unit not in raw_of:
-                raw_of[unit] = w_in.tile([P, PASSES, PACK, N_BLOCK], BF16, name="w_raw")
-            for g in passes:
+            raw_of[unit] = w_in.tile([P, PASSES, PACK, N_BLOCK], BF16, name="w_raw")
+            for g in range(PASSES):
                 nc.sync.dma_start(
                     out=raw_of[unit][:, g],
                     in_=We[e, K_PASS * g : K_PASS * (g + 1), N_BLOCK * j : N_BLOCK * (j + 1)].rearrange(
@@ -67,13 +67,12 @@ def tile_enhancedmathematicalreasoning_pa_kernel(tc, hidden_states, op_logits, W
 
         logits = keep.tile([P, TOKEN_TILES, E], BF16)
         nc.sync.dma_start(out=logits[:], in_=logit_rows)
-        load(0, passes=range(1))
+        load_x(0)
+        load(0)
         be_rows = keep.tile([P, HO], BF16)
         nc.vector.memset(be_rows[:], 0.0)
         for part in range(GATE_PARTS):
             nc.sync.dma_start(out=be_rows[E * part : E * (part + 1), :], in_=be)
-        load(0, passes=range(1, PASSES))
-        load_x(0)
         load_x(1)
         for unit in range(1, 5):
             load(unit)
@@ -148,7 +147,10 @@ def tile_enhancedmathematicalreasoning_pa_kernel(tc, hidden_states, op_logits, W
             return stage[:, start : start + PASSES * N_BLOCK, :]
 
         def shares(unit):
-            vector_cols, helper_cols = HEAD_COLS[unit] if unit < len(HEAD_COLS) else (0, HELPER_COLS)
+            if unit < len(HEAD_COLS):
+                vector_cols, helper_cols = HEAD_COLS[unit]
+            else:
+                vector_cols, helper_cols = BLOCK_0_VECTOR_COLS if unit < E else 0, HELPER_COLS
             cols = PASSES * N_BLOCK
             ends = [cols, cols - helper_cols, cols - helper_cols - vector_cols, 0]
             if unit % 2 == 1:
@@ -243,14 +245,12 @@ def tile_enhancedmathematicalreasoning_pa_kernel(tc, hidden_states, op_logits, W
         gate_t = keep.tile([P, TOKEN_TILES, P], BF16)
 
         def split_gate():
-            rest = gate
-            for part in range(GATE_PARTS):
-                kept = gate_parts[:, :, E * part : E * (part + 1)]
-                nc.vector.tensor_copy(out=kept, in_=rest[:])
-                if part < GATE_PARTS - 1:
-                    smaller = keep.tile([P, TOKEN_TILES, E], F32, name="rest%d" % part)
-                    nc.vector.tensor_tensor(out=smaller[:], in0=rest[:], in1=kept, op=ALU.subtract)
-                    rest = smaller
+            kept = [gate_parts[:, :, E * part : E * (part + 1)] for part in range(GATE_PARTS)]
+            rest = keep.tile([P, TOKEN_TILES, E], F32)
+            nc.vector.tensor_copy(out=kept[0], in_=gate[:])
+            nc.vector.tensor_tensor(out=rest[:], in0=gate[:], in1=kept[0], op=ALU.subtract)
+            nc.vector.tensor_copy(out=kept[1], in_=rest[:])
+            nc.vector.tensor_tensor(out=kept[2], in0=rest[:], in1=kept[1], op=ALU.subtract)
 
         def turn_gate():
             bank = psum.tile([P, TOKEN_TILES, P], BF16, tag="bank")
@@ -272,18 +272,18 @@ def tile_enhancedmathematicalreasoning_pa_kernel(tc, hidden_states, op_logits, W
             for i, bank in bias_banks.items():
                 nc.scalar.copy(out=total[:, i, n_cols], in_=bank[:])
 
+        x_banks = turn_x(0)
         split_gate()
         gate_t_bank = turn_gate()
-        regroup(0)
+        group_x(0, x_banks)
         nc.vector.tensor_copy(out=gate_t[:], in_=gate_t_bank[:])
+        regroup(0)
+        quantize_x(0)
         regroup_on_vector(0)
         bias_banks = multiply_bias(0)
         start_sum(0, bias_banks)
         codes = quantize(0)
-        x_banks = turn_x(0)
-        group_x(0, x_banks)
         x_banks = turn_x(1)
-        quantize_x(0)
         group_x(1, x_banks)
         multiply(0, *codes, tiles=range(2))
         regroup(1)

@@ -25,7 +25,7 @@ UNITS = N_BLOCKS * E
 RUN = 4
 HELPER_COLS = 256
 HEAD_COLS = ((512, 0), (448, 64), (256, 128))
-BLOCK_0_VECTOR_COLS = 32
+TENSOR_COLS = 128
 SCALAR_COLS = PASSES * N_BLOCK - HELPER_COLS
 BIAS_UNITS = (2, 4, 6, 8)
 TAIL_TILE = 3
@@ -43,7 +43,7 @@ def tile_enhancedmathematicalreasoning_pa_kernel(tc, hidden_states, op_logits, W
 
     with tc.tile_pool(name="keep", bufs=1) as keep, tc.tile_pool(name="w_in", bufs=6) as w_in, tc.tile_pool(
         name="w_mx", bufs=2
-    ) as w_mx, tc.psum_pool(name="psum", bufs=8) as psum, tc.manual_schedule():
+    ) as w_mx, tc.psum_pool(name="psum", bufs=7) as psum, tc.psum_pool(name="psum_turn", bufs=1) as psum_turn, tc.manual_schedule():
         x_raw = keep.tile([P, TOKEN_TILES, H], BF16)
         raw_of = {}
         banks_of = {}
@@ -148,14 +148,15 @@ def tile_enhancedmathematicalreasoning_pa_kernel(tc, hidden_states, op_logits, W
 
         def shares(unit):
             if unit < len(HEAD_COLS):
-                vector_cols, helper_cols = HEAD_COLS[unit]
+                (vector_cols, helper_cols), tensor_cols = HEAD_COLS[unit], 0
             else:
-                vector_cols, helper_cols = BLOCK_0_VECTOR_COLS if unit < E else 0, HELPER_COLS
+                vector_cols, helper_cols, tensor_cols = 0, HELPER_COLS, TENSOR_COLS
             cols = PASSES * N_BLOCK
-            ends = [cols, cols - helper_cols, cols - helper_cols - vector_cols, 0]
+            ends = [cols, cols - helper_cols, cols - helper_cols - vector_cols, tensor_cols]
             if unit % 2 == 1:
                 ends = [cols - end for end in ends]
-            return [(min(pair), max(pair)) for pair in zip(ends[2::-1], ends[:0:-1])]
+            tensor_share = sorted((ends[3], cols if unit % 2 == 1 else 0))
+            return [(min(pair), max(pair)) for pair in zip(ends[2::-1], ends[:0:-1])] + [tuple(tensor_share)]
 
         def cut(share):
             found = []
@@ -182,6 +183,27 @@ def tile_enhancedmathematicalreasoning_pa_kernel(tc, hidden_states, op_logits, W
                     scalar2=0.0,
                     op0=ALU.mult,
                     op1=ALU.add,
+                )
+
+        def turn_cols(unit):
+            turned = []
+            for g, cols, both_cols in cut(shares(unit)[3]):
+                bank = psum_turn.tile([P, TENSOR_COLS, PACK], BF16, tag="turn")
+                nc.tensor.matmul(
+                    bank[:].rearrange("p c t -> p t c"),
+                    lhsT=identity_bf16[:],
+                    rhs=raw_of[unit][:, g, :, cols],
+                    start=True,
+                    stop=True,
+                )
+                turned.append((bank, both_cols))
+            return turned
+
+        def fetch_turned(unit, turned):
+            for bank, both_cols in turned:
+                nc.scalar.copy(
+                    out=grouped(unit)[:, both_cols, :].rearrange("p c t -> p (c t)"),
+                    in_=bank[:].rearrange("p c t -> p (c t)"),
                 )
 
         def regroup_on_vector(unit):
@@ -294,10 +316,12 @@ def tile_enhancedmathematicalreasoning_pa_kernel(tc, hidden_states, op_logits, W
 
         for unit in range(1, UNITS):
             codes = quantize(unit)
+            turned = turn_cols(unit + 1) if unit + 1 < UNITS else []
             if unit in BIAS_UNITS:
                 bias_banks = multiply_bias(1, tiles=(BIAS_UNITS.index(unit),))
             if unit + 1 < UNITS:
                 regroup(unit + 1)
+                fetch_turned(unit + 1, turned)
                 regroup_on_vector(unit + 1)
             if unit + 4 < UNITS:
                 load(unit + 4)

@@ -22,7 +22,7 @@ TOKEN_TILES = TOKENS // P
 N_BLOCK = 512
 N_BLOCKS = HO // N_BLOCK
 UNITS = N_BLOCKS * E
-RUN = 4
+RUN = 8
 HELPER_COLS = 256
 HEAD_COLS = ((512, 0), (448, 64), (256, 128))
 TENSOR_COLS = 128

@@ -24,8 +24,10 @@ N_BLOCKS = HO // N_BLOCK
 UNITS = N_BLOCKS * E
 RUN = 8
 HELPER_COLS = 256
-HEAD_COLS = ((512, 0), (448, 64), (256, 128))
+HEAD_COLS = ((512, 0, 0), (448, 0, 192), (64, 192, 256))
 TENSOR_COLS = 128
+BANK_COLS = 256
+TURN_COLS = 128
 SCALAR_COLS = PASSES * N_BLOCK - HELPER_COLS
 BIAS_UNITS = (2, 4, 6, 8)
 TAIL_TILE = 3
@@ -148,7 +150,7 @@ def tile_enhancedmathematicalreasoning_pa_kernel(tc, hidden_states, op_logits, W
 
         def shares(unit):
             if unit < len(HEAD_COLS):
-                (vector_cols, helper_cols), tensor_cols = HEAD_COLS[unit], 0
+                vector_cols, helper_cols, tensor_cols = HEAD_COLS[unit]
             else:
                 vector_cols, helper_cols, tensor_cols = 0, HELPER_COLS, TENSOR_COLS
             cols = PASSES * N_BLOCK
@@ -188,22 +190,25 @@ def tile_enhancedmathematicalreasoning_pa_kernel(tc, hidden_states, op_logits, W
         def turn_cols(unit):
             turned = []
             for g, cols, both_cols in cut(shares(unit)[3]):
-                bank = psum_turn.tile([P, TENSOR_COLS, PACK], BF16, tag="turn")
-                nc.tensor.matmul(
-                    bank[:].rearrange("p c t -> p t c"),
-                    lhsT=identity_bf16[:],
-                    rhs=raw_of[unit][:, g, :, cols],
-                    start=True,
-                    stop=True,
-                )
-                turned.append((bank, both_cols))
+                n_cols = cols.stop - cols.start
+                bank = psum_turn.tile([P, BANK_COLS, PACK], BF16, tag="turn")
+                for first in range(0, n_cols, TURN_COLS):
+                    last = min(first + TURN_COLS, n_cols)
+                    nc.tensor.matmul(
+                        bank[:, first:last, :].rearrange("p c t -> p t c"),
+                        lhsT=identity_bf16[:],
+                        rhs=raw_of[unit][:, g, :, cols.start + first : cols.start + last],
+                        start=True,
+                        stop=True,
+                    )
+                turned.append((bank[:, 0:n_cols, :], both_cols))
             return turned
 
         def fetch_turned(unit, turned):
             for bank, both_cols in turned:
                 nc.scalar.copy(
                     out=grouped(unit)[:, both_cols, :].rearrange("p c t -> p (c t)"),
-                    in_=bank[:].rearrange("p c t -> p (c t)"),
+                    in_=bank.rearrange("p c t -> p (c t)"),
                 )
 
         def regroup_on_vector(unit):
@@ -221,6 +226,8 @@ def tile_enhancedmathematicalreasoning_pa_kernel(tc, hidden_states, op_logits, W
             return w_codes, w_scales
 
         def tile_order(unit):
+            if unit == UNITS - 1:
+                return (TAIL_TILE,) + tuple(range(TAIL_TILE))
             return range(TOKEN_TILES) if unit % 2 == 0 else range(TOKEN_TILES - 1, -1, -1)
 
         def multiply(unit, w_codes, w_scales, tiles=None):
@@ -266,12 +273,12 @@ def tile_enhancedmathematicalreasoning_pa_kernel(tc, hidden_states, op_logits, W
 
         gate_t = keep.tile([P, TOKEN_TILES, P], BF16)
 
+        kept = [gate_parts[:, :, E * part : E * (part + 1)] for part in range(GATE_PARTS)]
+        rest = keep.tile([P, TOKEN_TILES, E], F32)
+
         def split_gate():
-            kept = [gate_parts[:, :, E * part : E * (part + 1)] for part in range(GATE_PARTS)]
-            rest = keep.tile([P, TOKEN_TILES, E], F32)
-            nc.vector.tensor_copy(out=kept[0], in_=gate[:])
+            nc.vector.tensor_tensor(out=kept[1], in0=gate[:], in1=kept[0], op=ALU.subtract)
             nc.vector.tensor_tensor(out=rest[:], in0=gate[:], in1=kept[0], op=ALU.subtract)
-            nc.vector.tensor_copy(out=kept[1], in_=rest[:])
             nc.vector.tensor_tensor(out=kept[2], in0=rest[:], in1=kept[1], op=ALU.subtract)
 
         def turn_gate():
@@ -295,12 +302,13 @@ def tile_enhancedmathematicalreasoning_pa_kernel(tc, hidden_states, op_logits, W
                 nc.scalar.copy(out=total[:, i, n_cols], in_=bank[:])
 
         x_banks = turn_x(0)
+        nc.vector.tensor_copy(out=kept[0], in_=gate[:])
+        group_x(0, x_banks)
         split_gate()
         gate_t_bank = turn_gate()
-        group_x(0, x_banks)
+        quantize_x(0)
         nc.vector.tensor_copy(out=gate_t[:], in_=gate_t_bank[:])
         regroup(0)
-        quantize_x(0)
         regroup_on_vector(0)
         bias_banks = multiply_bias(0)
         start_sum(0, bias_banks)
@@ -308,7 +316,9 @@ def tile_enhancedmathematicalreasoning_pa_kernel(tc, hidden_states, op_logits, W
         x_banks = turn_x(1)
         group_x(1, x_banks)
         multiply(0, *codes, tiles=range(2))
+        turned = turn_cols(1)
         regroup(1)
+        fetch_turned(1, turned)
         regroup_on_vector(1)
         quantize_x(1)
         multiply(0, *codes, tiles=range(2, 4))
@@ -322,13 +332,14 @@ def tile_enhancedmathematicalreasoning_pa_kernel(tc, hidden_states, op_logits, W
             if unit + 1 < UNITS:
                 regroup(unit + 1)
                 fetch_turned(unit + 1, turned)
-                regroup_on_vector(unit + 1)
             if unit + 4 < UNITS:
                 load(unit + 4)
             if unit in BIAS_UNITS:
                 start_sum(1, bias_banks)
             multiply(unit, *codes)
             add_up(unit - 1, tiles=range(2, 4) if unit == 1 else None)
+            if unit + 1 < UNITS:
+                regroup_on_vector(unit + 1)
         add_up(UNITS - 1)
         n_cols = slice(N_BLOCK * (N_BLOCKS - 1), HO)
         nc.sync.dma_start(out=out_rows[:, TAIL_TILE, n_cols], in_=total[:, TAIL_TILE, n_cols])

@@ -32,6 +32,7 @@ SCALAR_COLS = PASSES * N_BLOCK - HELPER_COLS
 BIAS_UNITS = (2, 4, 6, 8)
 TAIL_TILE = 3
 TAIL_UNITS = (UNITS - 2, UNITS - 1)
+WARM_UPS = 6, 2, 2, 1, 1
 GATE_PARTS = 3
 
 FLOPS = 2 * TOKENS * H * HO * E
@@ -71,6 +72,8 @@ def tile_enhancedmathematicalreasoning_pa_kernel(tc, hidden_states, op_logits, W
         nc.sync.dma_start(out=logits[:], in_=logit_rows)
         load_x(0)
         load(0)
+        zeros = keep.tile([P, N_BLOCK], BF16)
+        nc.vector.memset(zeros[:], 0.0)
         be_rows = keep.tile([P, HO], BF16)
         nc.vector.memset(be_rows[:], 0.0)
         for part in range(GATE_PARTS):
@@ -301,11 +304,19 @@ def tile_enhancedmathematicalreasoning_pa_kernel(tc, hidden_states, op_logits, W
             for i, bank in bias_banks.items():
                 nc.scalar.copy(out=total[:, i, n_cols], in_=bank[:])
 
+        def keep_warm(times):
+            bank = psum.tile([P, N_BLOCK], F32, tag="bank")
+            for i in range(times):
+                nc.tensor.matmul(bank[:], lhsT=zeros[:, 0:P], rhs=zeros[:], start=True, stop=True)
+
+        keep_warm(WARM_UPS[0])
         x_banks = turn_x(0)
+        keep_warm(WARM_UPS[1])
         nc.vector.tensor_copy(out=kept[0], in_=gate[:])
         group_x(0, x_banks)
         split_gate()
         gate_t_bank = turn_gate()
+        keep_warm(WARM_UPS[2])
         quantize_x(0)
         nc.vector.tensor_copy(out=gate_t[:], in_=gate_t_bank[:])
         regroup(0)
@@ -313,7 +324,9 @@ def tile_enhancedmathematicalreasoning_pa_kernel(tc, hidden_states, op_logits, W
         bias_banks = multiply_bias(0)
         start_sum(0, bias_banks)
         codes = quantize(0)
+        keep_warm(WARM_UPS[3])
         x_banks = turn_x(1)
+        keep_warm(WARM_UPS[4])
         group_x(1, x_banks)
         multiply(0, *codes, tiles=range(2))
         turned = turn_cols(1)

@@ -233,8 +233,11 @@ def tile_enhancedmathematicalreasoning_pa_kernel(tc, hidden_states, op_logits, W
                 return (TAIL_TILE,) + tuple(range(TAIL_TILE))
             return range(TOKEN_TILES) if unit % 2 == 0 else range(TOKEN_TILES - 1, -1, -1)
 
+        def product_order(unit):
+            return tile_order(unit) if unit == UNITS - 1 else tuple(reversed(tile_order(unit)))
+
         def multiply(unit, w_codes, w_scales, tiles=None):
-            for i in tiles or tile_order(unit):
+            for i in tiles or product_order(unit):
                 half, t_cols = i // 2, slice(P * (i % 2), P * (i % 2 + 1))
                 product = psum.tile([P, N_BLOCK], F32, tag="bank")
                 for g in range(PASSES):
@@ -280,8 +283,8 @@ def tile_enhancedmathematicalreasoning_pa_kernel(tc, hidden_states, op_logits, W
         rest = keep.tile([P, TOKEN_TILES, E], F32)
 
         def split_gate():
-            nc.vector.tensor_tensor(out=kept[1], in0=gate[:], in1=kept[0], op=ALU.subtract)
             nc.vector.tensor_tensor(out=rest[:], in0=gate[:], in1=kept[0], op=ALU.subtract)
+            nc.vector.tensor_tensor(out=kept[1], in0=gate[:], in1=kept[0], op=ALU.subtract)
             nc.vector.tensor_tensor(out=kept[2], in0=rest[:], in1=kept[1], op=ALU.subtract)
 
         def turn_gate():

@@ -23,9 +23,9 @@ N_BLOCK = 512
 N_BLOCKS = HO // N_BLOCK
 UNITS = N_BLOCKS * E
 RUN = 8
-HELPER_COLS = 256
+HELPER_COLS = 192
 HEAD_COLS = ((512, 0, 0), (448, 0, 192), (64, 192, 256))
-TENSOR_COLS = 128
+TENSOR_COLS = 192
 BANK_COLS = 256
 TURN_COLS = 128
 SCALAR_COLS = PASSES * N_BLOCK - HELPER_COLS
@@ -33,6 +33,8 @@ BIAS_UNITS = (2, 4, 6, 8)
 TAIL_TILE = 3
 TAIL_UNITS = (UNITS - 2, UNITS - 1)
 WARM_UPS = 6, 2, 2, 1, 1
+HELPED_UNITS = range(4, UNITS - 1)
+HELPED_COLS = 128
 GATE_PARTS = 3
 
 FLOPS = 2 * TOKENS * H * HO * E
@@ -231,7 +233,7 @@ def tile_enhancedmathematicalreasoning_pa_kernel(tc, hidden_states, op_logits, W
         def tile_order(unit):
             if unit == UNITS - 1:
                 return (TAIL_TILE,) + tuple(range(TAIL_TILE))
-            return range(TOKEN_TILES) if unit % 2 == 0 else range(TOKEN_TILES - 1, -1, -1)
+            return tuple(range(TOKEN_TILES)) if unit % 2 == 0 else tuple(range(TOKEN_TILES - 1, -1, -1))
 
         def product_order(unit):
             return tile_order(unit) if unit == UNITS - 1 else tuple(reversed(tile_order(unit)))
@@ -252,25 +254,37 @@ def tile_enhancedmathematicalreasoning_pa_kernel(tc, hidden_states, op_logits, W
                     )
                 banks_of[unit, i] = product
 
+        def helped_tile(unit):
+            return tile_order(unit)[-1] if unit + 1 in HELPED_UNITS else None
+
+        def weigh(unit, i, n_cols):
+            e = unit % E
+            weighted = w_mx.tile([P, n_cols], F32, name="weighted%d" % n_cols)
+            nc.scalar.activation(
+                out=weighted[:], in_=banks_of[unit, i][:, 0:n_cols], func=ACT.Copy, scale=gate[:, i, e : e + 1]
+            )
+            return weighted
+
+        def help_add(unit, i, weighted):
+            start = N_BLOCK * (unit // E)
+            n_cols = slice(start, start + weighted.shape[1])
+            nc.gpsimd.tensor_tensor(out=total[:, i, n_cols], in0=weighted[:], in1=total[:, i, n_cols], op=ALU.add)
+
         def add_up(unit, tiles=None):
             j, e = divmod(unit, E)
             n_cols = slice(N_BLOCK * j, N_BLOCK * (j + 1))
             for i in tiles or tile_order(unit):
                 if i == TAIL_TILE and unit in TAIL_UNITS:
-                    weighted = keep.tile([P, N_BLOCK], F32, name="weighted%d" % unit)
-                    nc.scalar.activation(
-                        out=weighted[:], in_=banks_of[unit, i][:], func=ACT.Copy, scale=gate[:, i, e : e + 1]
-                    )
                     wait_for_quantize(UNITS - 1)
-                    nc.gpsimd.tensor_tensor(
-                        out=total[:, i, n_cols], in0=weighted[:], in1=total[:, i, n_cols], op=ALU.add
-                    )
+                    help_add(unit, i, weigh(unit, i, N_BLOCK))
                 else:
+                    first_col = HELPED_COLS if i == helped_tile(unit) else 0
+                    sum_cols = slice(N_BLOCK * j + first_col, N_BLOCK * (j + 1))
                     nc.vector.scalar_tensor_tensor(
-                        out=total[:, i, n_cols],
-                        in0=banks_of[unit, i][:],
+                        out=total[:, i, sum_cols],
+                        in0=banks_of[unit, i][:, first_col:],
                         scalar=gate[:, i, e : e + 1],
-                        in1=total[:, i, n_cols],
+                        in1=total[:, i, sum_cols],
                         op0=ALU.mult,
                         op1=ALU.add,
                     )
@@ -345,6 +359,9 @@ def tile_enhancedmathematicalreasoning_pa_kernel(tc, hidden_states, op_logits, W
             turned = turn_cols(unit + 1) if unit + 1 < UNITS else []
             if unit in BIAS_UNITS:
                 bias_banks = multiply_bias(1, tiles=(BIAS_UNITS.index(unit),))
+            helped = helped_tile(unit - 1)
+            if helped is not None:
+                weighted = weigh(unit - 1, helped, HELPED_COLS)
             if unit + 1 < UNITS:
                 regroup(unit + 1)
                 fetch_turned(unit + 1, turned)
@@ -353,6 +370,8 @@ def tile_enhancedmathematicalreasoning_pa_kernel(tc, hidden_states, op_logits, W
             if unit in BIAS_UNITS:
                 start_sum(1, bias_banks)
             multiply(unit, *codes)
+            if helped is not None:
+                help_add(unit - 1, helped, weighted)
             add_up(unit - 1, tiles=range(2, 4) if unit == 1 else None)
             if unit + 1 < UNITS:
                 regroup_on_vector(unit + 1)

@@ -25,7 +25,6 @@ UNITS = N_BLOCKS * E
 RUN = 8
 HELPER_COLS = 192
 HEAD_COLS = ((512, 0, 0), (448, 0, 192), (64, 192, 256))
-TENSOR_COLS = 192
 BANK_COLS = 256
 TURN_COLS = 128
 SCALAR_COLS = PASSES * N_BLOCK - HELPER_COLS
@@ -33,7 +32,9 @@ BIAS_UNITS = (2, 4, 6, 8)
 TAIL_TILE = 3
 TAIL_UNITS = (UNITS - 2, UNITS - 1)
 WARM_UPS = 6, 2, 2, 1, 1
-HELPED_UNITS = range(4, UNITS - 1)
+HELPED_UNITS = range(E + 1, UNITS - 1)
+EARLY_COLS = (256, 160)
+LATE_COLS = (192, 192)
 HELPED_COLS = 128
 GATE_PARTS = 3
 
@@ -157,7 +158,7 @@ def tile_enhancedmathematicalreasoning_pa_kernel(tc, hidden_states, op_logits, W
             if unit < len(HEAD_COLS):
                 vector_cols, helper_cols, tensor_cols = HEAD_COLS[unit]
             else:
-                vector_cols, helper_cols, tensor_cols = 0, HELPER_COLS, TENSOR_COLS
+                vector_cols, helper_cols, tensor_cols = 0, *(LATE_COLS if unit - 1 in HELPED_UNITS else EARLY_COLS)
             cols = PASSES * N_BLOCK
             ends = [cols, cols - helper_cols, cols - helper_cols - vector_cols, tensor_cols]
             if unit % 2 == 1:

import concourse.mybir as mybir
from concourse.masks import make_identity

F32 = mybir.dt.float32
BF16 = mybir.dt.bfloat16
U32 = mybir.dt.uint32
U8 = mybir.dt.uint8
FP8X4 = mybir.dt.float8_e4m3fn_x4
ALU = mybir.AluOpType
ACT = mybir.ActivationFunctionType
AXIS = mybir.AxisListType

P = 128
PACK = 4
K_PASS = P * PACK
TOKENS = 512
H = 1024
HO = 1024
E = 8
PASSES = H // K_PASS
TOKEN_TILES = TOKENS // P
N_BLOCK = 512
N_BLOCKS = HO // N_BLOCK
UNITS = N_BLOCKS * E
RUN = 8
HELPER_COLS = 192
HEAD_COLS = ((512, 0, 0), (448, 0, 192), (64, 192, 256))
BANK_COLS = 256
TURN_COLS = 128
SCALAR_COLS = PASSES * N_BLOCK - HELPER_COLS
BIAS_UNITS = (2, 4, 6, 8)
TAIL_TILE = 3
TAIL_UNITS = (UNITS - 2, UNITS - 1)
WARM_UPS = 6, 2, 2, 1, 1
HELPED_UNITS = range(E + 1, UNITS - 1)
EARLY_COLS = (256, 160)
LATE_COLS = (192, 192)
HELPED_COLS = 128
GATE_PARTS = 3

FLOPS = 2 * TOKENS * H * HO * E


def tile_enhancedmathematicalreasoning_pa_kernel(tc, hidden_states, op_logits, We, be, out):
    nc = tc.nc
    x_rows = hidden_states.flatten_outer_dims().rearrange("(p i) k -> p i k", i=TOKEN_TILES)
    logit_rows = op_logits.flatten_outer_dims().rearrange("(p i) e -> p i e", i=TOKEN_TILES)
    out_rows = out.flatten_outer_dims().rearrange("(p i) n -> p i n", i=TOKEN_TILES)

    with tc.tile_pool(name="keep", bufs=1) as keep, tc.tile_pool(name="w_in", bufs=6) as w_in, tc.tile_pool(
        name="w_mx", bufs=2
    ) as w_mx, tc.psum_pool(name="psum", bufs=7) as psum, tc.psum_pool(name="psum_turn", bufs=1) as psum_turn, tc.manual_schedule():
        x_raw = keep.tile([P, TOKEN_TILES, H], BF16)
        raw_of = {}
        banks_of = {}
        codes_of = {}
        last_word = keep.tile([P, 1], U32)

        def load_x(half):
            tiles = slice(2 * half, 2 * half + 2)
            nc.sync.dma_start(out=x_raw[:, tiles, :], in_=x_rows[:, tiles, :])

        def load(unit):
            j, e = divmod(unit, E)
            raw_of[unit] = w_in.tile([P, PASSES, PACK, N_BLOCK], BF16, name="w_raw")
            for g in range(PASSES):
                nc.sync.dma_start(
                    out=raw_of[unit][:, g],
                    in_=We[e, K_PASS * g : K_PASS * (g + 1), N_BLOCK * j : N_BLOCK * (j + 1)].rearrange(
                        "(p t) n -> p t n", t=PACK
                    ),
                )

        logits = keep.tile([P, TOKEN_TILES, E], BF16)
        nc.sync.dma_start(out=logits[:], in_=logit_rows)
        load_x(0)
        load(0)
        zeros = keep.tile([P, N_BLOCK], BF16)
        nc.vector.memset(zeros[:], 0.0)
        be_rows = keep.tile([P, HO], BF16)
        nc.vector.memset(be_rows[:], 0.0)
        for part in range(GATE_PARTS):
            nc.sync.dma_start(out=be_rows[E * part : E * (part + 1), :], in_=be)
        load_x(1)
        for unit in range(1, 5):
            load(unit)
        identity_f32 = keep.tile([P, P], F32)
        make_identity(nc, identity_f32[:])
        identity_bf16 = keep.tile([P, P], BF16)
        make_identity(nc, identity_bf16[:])
        gate_parts = keep.tile([P, TOKEN_TILES, P], BF16)
        nc.gpsimd.memset(gate_parts[:], 0.0)

        row_max = keep.tile([P, TOKEN_TILES], F32)
        nc.vector.tensor_reduce(out=row_max[:], in_=logits[:], axis=AXIS.X, op=ALU.max)
        shifted = keep.tile([P, TOKEN_TILES, E], F32)
        nc.vector.tensor_tensor(
            out=shifted[:],
            in0=logits[:],
            in1=row_max[:].unsqueeze(2).to_broadcast([P, TOKEN_TILES, E]),
            op=ALU.subtract,
        )
        exps = keep.tile([P, TOKEN_TILES, E], F32)
        nc.scalar.activation(out=exps[:], in_=shifted[:], func=ACT.Exp)
        row_sum = keep.tile([P, TOKEN_TILES], F32)
        nc.vector.tensor_reduce(out=row_sum[:], in_=exps[:], axis=AXIS.X, op=ALU.add)
        inv_sum = keep.tile([P, TOKEN_TILES], F32)
        nc.vector.reciprocal(out=inv_sum[:], in_=row_sum[:])
        gate = keep.tile([P, TOKEN_TILES, E], F32)
        nc.vector.tensor_tensor(
            out=gate[:],
            in0=exps[:],
            in1=inv_sum[:].unsqueeze(2).to_broadcast([P, TOKEN_TILES, E]),
            op=ALU.mult,
        )

        x_words = x_raw[:].bitcast(F32).rearrange("p i (g q u) -> p i g u q", g=PASSES, u=2)
        x_grouped = keep.tile([P, 2, PASSES, 2 * P, PACK], BF16, align_bytes=64)
        x_grouped_words = x_grouped[:].bitcast(F32)
        x_codes = keep.tile([P, 2, PASSES, 2 * P], U32, align_bytes=64)
        x_scales = keep.tile([P, 2, PASSES, 2 * P], U8, align_bytes=64)

        def turn_x(half):
            banks = []
            for g in range(PASSES):
                planes = psum.tile([P, 2, 2 * P], F32, tag="bank")
                for u in range(2):
                    for i in range(2):
                        nc.tensor.transpose(
                            planes[:, u, P * i : P * (i + 1)], x_words[:, 2 * half + i, g, u, :], identity_f32[:]
                        )
                banks.append(planes)
            return banks

        def group_x(half, banks):
            for g, copy in enumerate((nc.vector.tensor_copy, nc.scalar.copy)):
                copy(out=x_grouped_words[:, half, g], in_=banks[g][:].rearrange("p u r -> p r u"))

        def quantize_x(half):
            nc.vector.quantize_mx(
                out=x_codes[:, half].rearrange("p g r -> p (g r)").bitcast(FP8X4),
                scales=x_scales[:, half].rearrange("p g r -> p (g r)"),
                in_=x_grouped[:, half].rearrange("p g r t -> p (g r t)"),
            )

        def wait_for_quantize(unit):
            nc.gpsimd.tensor_copy(out=last_word[:], in_=codes_of[unit][:, 0, 0:1])

        total = keep.tile([P, TOKEN_TILES, HO], F32)

        stage = keep.tile([P, SCALAR_COLS + PASSES * N_BLOCK, PACK], BF16, align_bytes=64)

        def grouped(unit):
            start = SCALAR_COLS * (unit % 2)
            return stage[:, start : start + PASSES * N_BLOCK, :]

        def shares(unit):
            if unit < len(HEAD_COLS):
                vector_cols, helper_cols, tensor_cols = HEAD_COLS[unit]
            else:
                vector_cols, helper_cols, tensor_cols = 0, *(LATE_COLS if unit - 1 in HELPED_UNITS else EARLY_COLS)
            cols = PASSES * N_BLOCK
            ends = [cols, cols - helper_cols, cols - helper_cols - vector_cols, tensor_cols]
            if unit % 2 == 1:
                ends = [cols - end for end in ends]
            tensor_share = sorted((ends[3], cols if unit % 2 == 1 else 0))
            return [(min(pair), max(pair)) for pair in zip(ends[2::-1], ends[:0:-1])] + [tuple(tensor_share)]

        def cut(share):
            found = []
            for g in range(PASSES):
                start, end = max(share[0], N_BLOCK * g), min(share[1], N_BLOCK * (g + 1))
                if start < end:
                    found.append((g, slice(start - N_BLOCK * g, end - N_BLOCK * g), slice(start, end)))
            return found

        def copy_cols(copy, unit, share):
            for g, cols, both_cols in cut(share):
                copy(
                    out=grouped(unit)[:, both_cols, :].rearrange("p (c i) t -> p c t i", i=RUN),
                    in_=raw_of[unit][:, g, :, cols].rearrange("p t (c i) -> p c t i", i=RUN),
                )

        def regroup(unit):
            copy_cols(nc.scalar.copy, unit, shares(unit)[0])
            for g, cols, both_cols in cut(shares(unit)[2]):
                nc.gpsimd.tensor_scalar(
                    out=grouped(unit)[:, both_cols, :],
                    in0=raw_of[unit][:, g, :, cols].rearrange("p t n -> p n t"),
                    scalar1=1.0,
                    scalar2=0.0,
                    op0=ALU.mult,
                    op1=ALU.add,
                )

        def turn_cols(unit):
            turned = []
            for g, cols, both_cols in cut(shares(unit)[3]):
                n_cols = cols.stop - cols.start
                bank = psum_turn.tile([P, BANK_COLS, PACK], BF16, tag="turn")
                for first in range(0, n_cols, TURN_COLS):
                    last = min(first + TURN_COLS, n_cols)
                    nc.tensor.matmul(
                        bank[:, first:last, :].rearrange("p c t -> p t c"),
                        lhsT=identity_bf16[:],
                        rhs=raw_of[unit][:, g, :, cols.start + first : cols.start + last],
                        start=True,
                        stop=True,
                    )
                turned.append((bank[:, 0:n_cols, :], both_cols))
            return turned

        def fetch_turned(unit, turned):
            for bank, both_cols in turned:
                nc.scalar.copy(
                    out=grouped(unit)[:, both_cols, :].rearrange("p c t -> p (c t)"),
                    in_=bank.rearrange("p c t -> p (c t)"),
                )

        def regroup_on_vector(unit):
            copy_cols(nc.vector.tensor_copy, unit, shares(unit)[1])

        def quantize(unit):
            w_codes = w_mx.tile([P, PASSES, N_BLOCK], U32, align_bytes=64)
            w_scales = w_mx.tile([P, PASSES, N_BLOCK], U8, align_bytes=64)
            nc.vector.quantize_mx(
                out=w_codes[:].rearrange("p g n -> p (g n)").bitcast(FP8X4),
                scales=w_scales[:].rearrange("p g n -> p (g n)"),
                in_=grouped(unit).rearrange("p n t -> p (n t)"),
            )
            codes_of[unit] = w_codes
            return w_codes, w_scales

        def tile_order(unit):
            if unit == UNITS - 1:
                return (TAIL_TILE,) + tuple(range(TAIL_TILE))
            return tuple(range(TOKEN_TILES)) if unit % 2 == 0 else tuple(range(TOKEN_TILES - 1, -1, -1))

        def product_order(unit):
            return tile_order(unit) if unit == UNITS - 1 else tuple(reversed(tile_order(unit)))

        def multiply(unit, w_codes, w_scales, tiles=None):
            for i in tiles or product_order(unit):
                half, t_cols = i // 2, slice(P * (i % 2), P * (i % 2 + 1))
                product = psum.tile([P, N_BLOCK], F32, tag="bank")
                for g in range(PASSES):
                    nc.tensor.matmul_mx(
                        out=product[:],
                        lhsT=x_codes[:, half, g, t_cols].bitcast(FP8X4),
                        lhsT_scale=x_scales[:, half, g, t_cols],
                        rhs=w_codes[:, g, :].bitcast(FP8X4),
                        rhs_scale=w_scales[:, g, :],
                        start=(g == 0),
                        stop=(g == PASSES - 1),
                    )
                banks_of[unit, i] = product

        def helped_tile(unit):
            return tile_order(unit)[-1] if unit + 1 in HELPED_UNITS else None

        def weigh(unit, i, n_cols):
            e = unit % E
            weighted = w_mx.tile([P, n_cols], F32, name="weighted%d" % n_cols)
            nc.scalar.activation(
                out=weighted[:], in_=banks_of[unit, i][:, 0:n_cols], func=ACT.Copy, scale=gate[:, i, e : e + 1]
            )
            return weighted

        def help_add(unit, i, weighted):
            start = N_BLOCK * (unit // E)
            n_cols = slice(start, start + weighted.shape[1])
            nc.gpsimd.tensor_tensor(out=total[:, i, n_cols], in0=weighted[:], in1=total[:, i, n_cols], op=ALU.add)

        def add_up(unit, tiles=None):
            j, e = divmod(unit, E)
            n_cols = slice(N_BLOCK * j, N_BLOCK * (j + 1))
            for i in tiles or tile_order(unit):
                if i == TAIL_TILE and unit in TAIL_UNITS:
                    wait_for_quantize(UNITS - 1)
                    help_add(unit, i, weigh(unit, i, N_BLOCK))
                else:
                    first_col = HELPED_COLS if i == helped_tile(unit) else 0
                    sum_cols = slice(N_BLOCK * j + first_col, N_BLOCK * (j + 1))
                    nc.vector.scalar_tensor_tensor(
                        out=total[:, i, sum_cols],
                        in0=banks_of[unit, i][:, first_col:],
                        scalar=gate[:, i, e : e + 1],
                        in1=total[:, i, sum_cols],
                        op0=ALU.mult,
                        op1=ALU.add,
                    )
                if e == E - 1 and not (i == TAIL_TILE and unit in TAIL_UNITS):
                    nc.sync.dma_start(out=out_rows[:, i, n_cols], in_=total[:, i, n_cols])

        gate_t = keep.tile([P, TOKEN_TILES, P], BF16)

        kept = [gate_parts[:, :, E * part : E * (part + 1)] for part in range(GATE_PARTS)]
        rest = keep.tile([P, TOKEN_TILES, E], F32)

        def split_gate():
            nc.vector.tensor_tensor(out=rest[:], in0=gate[:], in1=kept[0], op=ALU.subtract)
            nc.vector.tensor_tensor(out=kept[1], in0=gate[:], in1=kept[0], op=ALU.subtract)
            nc.vector.tensor_tensor(out=kept[2], in0=rest[:], in1=kept[1], op=ALU.subtract)

        def turn_gate():
            bank = psum.tile([P, TOKEN_TILES, P], BF16, tag="bank")
            for i in range(TOKEN_TILES):
                nc.tensor.transpose(bank[:, i, :], gate_parts[:, i, :], identity_bf16[:])
            return bank

        def multiply_bias(j, tiles=range(TOKEN_TILES)):
            n_cols = slice(N_BLOCK * j, N_BLOCK * (j + 1))
            bias_banks = {}
            for i in tiles:
                bias_bank = psum.tile([P, N_BLOCK], F32, tag="bank")
                nc.tensor.matmul(bias_bank[:], lhsT=gate_t[:, i, :], rhs=be_rows[:, n_cols], start=True, stop=True)
                bias_banks[i] = bias_bank
            return bias_banks

        def start_sum(j, bias_banks):
            n_cols = slice(N_BLOCK * j, N_BLOCK * (j + 1))
            for i, bank in bias_banks.items():
                nc.scalar.copy(out=total[:, i, n_cols], in_=bank[:])

        def keep_warm(times):
            bank = psum.tile([P, N_BLOCK], F32, tag="bank")
            for i in range(times):
                nc.tensor.matmul(bank[:], lhsT=zeros[:, 0:P], rhs=zeros[:], start=True, stop=True)

        keep_warm(WARM_UPS[0])
        x_banks = turn_x(0)
        keep_warm(WARM_UPS[1])
        nc.vector.tensor_copy(out=kept[0], in_=gate[:])
        group_x(0, x_banks)
        split_gate()
        gate_t_bank = turn_gate()
        keep_warm(WARM_UPS[2])
        quantize_x(0)
        nc.vector.tensor_copy(out=gate_t[:], in_=gate_t_bank[:])
        regroup(0)
        regroup_on_vector(0)
        bias_banks = multiply_bias(0)
        start_sum(0, bias_banks)
        codes = quantize(0)
        keep_warm(WARM_UPS[3])
        x_banks = turn_x(1)
        keep_warm(WARM_UPS[4])
        group_x(1, x_banks)
        multiply(0, *codes, tiles=range(2))
        turned = turn_cols(1)
        regroup(1)
        fetch_turned(1, turned)
        regroup_on_vector(1)
        quantize_x(1)
        multiply(0, *codes, tiles=range(2, 4))
        add_up(0, tiles=range(2))

        for unit in range(1, UNITS):
            codes = quantize(unit)
            turned = turn_cols(unit + 1) if unit + 1 < UNITS else []
            if unit in BIAS_UNITS:
                bias_banks = multiply_bias(1, tiles=(BIAS_UNITS.index(unit),))
            helped = helped_tile(unit - 1)
            if helped is not None:
                weighted = weigh(unit - 1, helped, HELPED_COLS)
            if unit + 1 < UNITS:
                regroup(unit + 1)
                fetch_turned(unit + 1, turned)
            if unit + 4 < UNITS:
                load(unit + 4)
            if unit in BIAS_UNITS:
                start_sum(1, bias_banks)
            multiply(unit, *codes)
            if helped is not None:
                help_add(unit - 1, helped, weighted)
            add_up(unit - 1, tiles=range(2, 4) if unit == 1 else None)
            if unit + 1 < UNITS:
                regroup_on_vector(unit + 1)
        add_up(UNITS - 1)
        n_cols = slice(N_BLOCK * (N_BLOCKS - 1), HO)
        nc.sync.dma_start(out=out_rows[:, TAIL_TILE, n_cols], in_=total[:, TAIL_TILE, n_cols])
